import numpy as np
import ml_dtypes


def mxq(x, axis, fmt="e4m3"):
    dtype, down = {"e4m3": (ml_dtypes.float8_e4m3fn, 7), "e5m2": (ml_dtypes.float8_e5m2, 14)}[fmt]
    v = np.moveaxis(np.asarray(x, np.float32).astype(ml_dtypes.bfloat16).astype(np.float64), axis, -1)
    blocks = v.reshape(v.shape[:-1] + (-1, 32))
    amax = np.abs(blocks).max(-1, keepdims=True)
    byte = np.maximum(np.where(amax > 0, np.frexp(amax)[1] - 1 + 127, 0) - down, 1)
    scale = np.exp2(byte - 127.0)
    codes = (blocks / scale).astype(np.float32).astype(dtype).astype(np.float64)
    return np.moveaxis((codes * scale).reshape(v.shape), -1, axis)


WIDE = False


def mx_kscale(k):
    if not WIDE:
        return np.ones(k)
    levels = np.array([10, -10, 5, -5, 0])
    a = np.random.permutation(np.resize(levels, k // 512 * 4)).reshape(k // 512, 4)
    idx = np.arange(k)
    return np.exp2(a[idx // 512, idx % 128 // 32])


BF16 = ml_dtypes.bfloat16


def bf(x):
    return np.asarray(x, np.float32).astype(BF16)


def f64(x):
    return np.asarray(x).astype(np.float64)


B, I, H = 512, 512, 2048
K = I + H


def setup_inputs():
    s = mx_kscale(I)
    sk = np.concatenate([s, np.ones(H)])
    return {"x": bf(np.random.standard_normal((B, I)) * s),
            "h": bf(np.random.standard_normal((B, H))),
            "time_delta": bf(np.random.uniform(0.0, 1.0, (B, 1))),
            "W_mod": bf(np.random.standard_normal((K, H)) * 0.6 / np.sqrt(K) / sk[:, None]),
            "b_mod": bf(np.random.standard_normal(H) * 0.2),
            "W_tgt": bf(np.random.standard_normal((K, H)) * 0.6 / np.sqrt(K) / sk[:, None]),
            "b_tgt": bf(np.random.standard_normal(H) * 0.2),
            "log_tau": bf(np.random.standard_normal(H) * 0.2),
            "bias": bf(np.random.standard_normal(H) * 0.1)}


def reference(x, h, time_delta, W_mod, b_mod, W_tgt, b_tgt, log_tau, bias):
    hf = f64(h)
    combined = np.concatenate([f64(x), hf], axis=-1)
    cq = mxq(combined, 1, "e4m3")
    f = np.tanh((cq @ mxq(f64(W_mod), 0, "e4m3")) + f64(b_mod))
    a = np.tanh((cq @ mxq(f64(W_tgt), 0, "e4m3")) + f64(b_tgt))
    tau = np.exp(f64(log_tau))[None, :]
    tau_sys = tau / (1.0 + tau * np.abs(f))
    decay = np.exp(-f64(time_delta) / (tau_sys + 1e-6))
    h_new = decay * hf + (1.0 - decay) * (a + f64(bias))
    return h_new

@@ -1,0 +1,268 @@
+import math
+from contextlib import ExitStack
+
+import concourse.mybir as mybir
+from concourse.masks import make_identity
+
+F32 = mybir.dt.float32
+BF16 = mybir.dt.bfloat16
+U32 = mybir.dt.uint32
+U8 = mybir.dt.uint8
+FP8X4 = mybir.dt.float8_e4m3fn_x4
+ACT = mybir.ActivationFunctionType
+ALU = mybir.AluOpType
+
+P = 128
+B, I, H = 512, 512, 2048
+K = I + H
+PACK = 4
+K_PASS = P * PACK
+PASSES = K // K_PASS
+BT = B // P
+EPS = 1e-6
+FLOPS = 2 * 2 * B * K * H
+
+SLABS = (512, 512, 512, 512)
+S_PATTERN = "VSVVSVSVVS"
+PIECES = (512, 512, 512, 128)
+RAW_BUFS = 10
+GRP_BUFS = 4
+
+
+def tile_ltccell_kernel(
+    tc, x, h, time_delta, W_mod, b_mod, W_tgt, b_tgt, log_tau, bias, out
+):
+    nc = tc.nc
+    weights = (W_mod, W_tgt)
+    with ExitStack() as ctx:
+        const = ctx.enter_context(tc.tile_pool(name="const", bufs=1))
+        rawp = ctx.enter_context(tc.tile_pool(name="rawp", bufs=RAW_BUFS))
+        grpp = ctx.enter_context(tc.tile_pool(name="grpp", bufs=GRP_BUFS))
+        cgp = ctx.enter_context(tc.tile_pool(name="cgp", bufs=2))
+        wqp = ctx.enter_context(tc.tile_pool(name="wqp", bufs=2))
+        epi = ctx.enter_context(tc.tile_pool(name="epi", bufs=2))
+        psum = ctx.enter_context(tc.psum_pool(name="psum", bufs=2))
+
+        warm = const.tile([P, 1], F32, name="warm")
+        nc.vector.memset(warm[:], 0.0)
+        nc.scalar.activation(out=warm[:], in_=warm[:], func=ACT.Exp)
+
+        vecs = const.tile([P, P], BF16, name="vecs")
+        nc.vector.memset(vecs[:], 0.0)
+        for v, vec in enumerate((b_mod, b_tgt, log_tau, bias)):
+            nc.scalar.dma_start(
+                out=vecs[16 * v : 16 * v + 16, :],
+                in_=vec.rearrange("(r c) -> r c", c=P),
+            )
+        nc.scalar.dma_start(
+            out=vecs[64 : 64 + BT, :],
+            in_=time_delta.rearrange("(i c) o -> i (c o)", c=P),
+        )
+        ident_f = const.tile([P, P], F32, name="ident_f")
+        make_identity(nc, ident_f[:])
+        ident_b = const.tile([P, P], BF16, name="ident_b")
+        make_identity(nc, ident_b[:])
+
+        chunks = []
+        col0 = 0
+        for s, wd in enumerate(SLABS):
+            for g in range(PASSES):
+                for m in range(2):
+                    chunks.append((s, g, m, col0, wd))
+            col0 += wd
+
+        raws = {}
+
+        def load_chunk(n):
+            s, g, m, c0, wd = chunks[n]
+            raw = rawp.tile([P, PACK, wd], BF16, name="raw%d" % n, tag="raw")
+            nc.sync.dma_start(
+                out=raw[:],
+                in_=weights[m][K_PASS * g : K_PASS * (g + 1), c0 : c0 + wd].rearrange(
+                    "(p j) w -> p j w", j=PACK
+                ),
+            )
+            raws[n] = raw
+
+        cn = const.tile([P, BT, K], BF16, name="cn")
+
+        def load_c(g):
+            src = x if g == 0 else h[:, K_PASS * (g - 1) : K_PASS * g]
+            nc.sync.dma_start(
+                out=cn[:, :, K_PASS * g : K_PASS * (g + 1)],
+                in_=src.rearrange("(i p) k -> p i k", p=P),
+            )
+
+        load_chunk(0)
+        load_chunk(1)
+        for g in range(PASSES):
+            load_c(g)
+
+        pst = psum.tile([P, P], BF16, name="pst", tag="GT")
+        nc.tensor.transpose(pst[:], vecs[:], ident_b[:])
+        cst = const.tile([P, P], F32, name="cst")
+        nc.vector.tensor_copy(out=cst[:], in_=pst[:])
+        itau = const.tile([P, 16], F32, name="itau")
+        nc.scalar.activation(out=itau[:], in_=cst[:, 32:48], func=ACT.Exp, scale=-1.0)
+        t1n = const.tile([P, 16], F32, name="t1n")
+        nc.vector.tensor_scalar(
+            out=t1n[:], in0=itau[:], scalar1=-EPS, scalar2=-1.0, op0=ALU.mult, op1=ALU.add
+        )
+        nk0 = const.tile([P, 16], F32, name="nk0")
+        nc.vector.reciprocal(out=nk0[:], in_=t1n[:])
+        sqe = const.tile([P, 16], F32, name="sqe")
+        nc.vector.tensor_scalar(
+            out=sqe[:], in0=nk0[:], scalar1=-math.sqrt(EPS), scalar2=None, op0=ALU.mult
+        )
+        c1 = const.tile([P, 16], F32, name="c1")
+        nc.vector.scalar_tensor_tensor(
+            out=c1[:], in0=nk0[:], scalar=-1.0, in1=nk0[:], op0=ALU.mult, op1=ALU.mult
+        )
+        c0 = const.tile([P, 16], F32, name="c0")
+        nc.vector.tensor_tensor(out=c0[:], in0=nk0[:], in1=itau[:], op=ALU.mult)
+
+        cnf = cn[:].bitcast(F32).rearrange("p i (g q u) -> p i g u q", g=PASSES, u=2)
+        cq = []
+        cs = []
+        bank_tags = ("F", "A", "RT", "GT")
+        for g in range(PASSES):
+            cg = cgp.tile([P, B * PACK], BF16, name="cg%d" % g, tag="cg", align_bytes=64)
+            cgf = cg[:].bitcast(F32).rearrange("p (b u) -> p b u", u=2)
+            for half in range(2):
+                xt = psum.tile(
+                    [P, 2, 2, P], F32, name="xt%d_%d" % (g, half), tag=bank_tags[(2 * g + half) % 4]
+                )
+                for il in range(2):
+                    for u in range(2):
+                        nc.tensor.transpose(
+                            xt[:, u, il, :], cnf[:, 2 * half + il, g, u, :], ident_f[:]
+                        )
+                dst = cgf[:, 256 * half : 256 * half + 256, :]
+                src = xt[:].rearrange("p u i b -> p (i b) u")
+                if half == 0:
+                    nc.vector.tensor_copy(out=dst, in_=src)
+                else:
+                    nc.scalar.copy(out=dst, in_=src)
+            cqg = const.tile([P, B], U32, name="cq%d" % g, align_bytes=64)
+            csg = const.tile([P, B], U8, name="cs%d" % g, align_bytes=64)
+            nc.vector.quantize_mx(out=cqg[:].bitcast(FP8X4), scales=csg[:], in_=cg[:])
+            cq.append(cqg)
+            cs.append(csg)
+
+        grps = {}
+        wqs = {}
+
+        def regroup(n, cpos, pw, k):
+            grp = grpp.tile([P, pw, PACK], BF16, name="grp%d" % k, tag="grp", align_bytes=64)
+            dst = grp[:].rearrange("p (c i) t -> p c t i", i=4)
+            src = raws[n][:, :, cpos : cpos + pw].rearrange("p t (c i) -> p c t i", i=4)
+            if S_PATTERN[k % len(S_PATTERN)] == "S":
+                nc.scalar.copy(out=dst, in_=src)
+            else:
+                nc.vector.tensor_copy(out=dst, in_=src)
+            grps[k] = grp
+
+        def quantise(n, cpos, pw, k):
+            s, g, m, c0_, wd = chunks[n]
+            wq = wqp.tile([P, pw], U32, name="wq%d" % k, tag="wq%d_%d" % (m, g), align_bytes=64)
+            ws = wqp.tile([P, pw], U8, name="ws%d" % k, tag="ws%d_%d" % (m, g), align_bytes=64)
+            nc.vector.quantize_mx(
+                out=wq[:].bitcast(FP8X4),
+                scales=ws[:],
+                in_=grps[k][:].rearrange("p w t -> p (w t)"),
+            )
+            wqs[(s, g, m, cpos // pw)] = (wq, ws)
+
+        def round_(s, q, r, osb):
+            acc = []
+            for m in range(2):
+                ps = psum.tile([P, B], F32, name="ps%d_%d" % (m, r), tag=("F", "A")[m])
+                for g in range(PASSES):
+                    pw = PIECES[s]
+                    wq, ws = wqs[(s, g, m, P * q // pw)]
+                    o = P * q % pw
+                    nc.tensor.matmul_mx(
+                        out=ps[:],
+                        lhsT=wq[:, o : o + P].bitcast(FP8X4),
+                        lhsT_scale=ws[:, o : o + P],
+                        rhs=cq[g][:].bitcast(FP8X4),
+                        rhs_scale=cs[g][:],
+                        start=(g == 0),
+                        stop=(g == PASSES - 1),
+                    )
+                acc.append(ps)
+            u = epi.tile([P, B], F32, name="u%d" % r, tag="u")
+            nc.scalar.activation(out=u[:], in_=acc[0][:], func=ACT.Abs, bias=cst[:, r : r + 1])
+            nc.scalar.activation(out=u[:], in_=u[:], func=ACT.Tanh)
+            a = epi.tile([P, B], F32, name="a%d" % r, tag="a")
+            nc.scalar.activation(
+                out=a[:], in_=acc[1][:], func=ACT.Tanh, bias=cst[:, 16 + r : 17 + r]
+            )
+            sq = epi.tile([P, B], F32, name="sq%d" % r, tag="sq")
+            nc.scalar.activation(out=sq[:], in_=u[:], func=ACT.Square, scale=sqe[:, r : r + 1])
+            lin = epi.tile([P, B], F32, name="lin%d" % r, tag="lin")
+            nc.vector.tensor_scalar(
+                out=lin[:], in0=u[:], scalar1=c1[:, r : r + 1], scalar2=c0[:, r : r + 1],
+                op0=ALU.mult, op1=ALU.add,
+            )
+            gn = epi.tile([P, B], F32, name="gn%d" % r, tag="gn")
+            nc.vector.tensor_scalar(
+                out=gn[:], in0=a[:], scalar1=cst[:, 48 + r : 49 + r], scalar2=-1.0,
+                op0=ALU.add, op1=ALU.mult,
+            )
+            rt = psum.tile([P, BT, P], F32, name="rt%d" % r, tag="RT")
+            dt = psum.tile([P, BT, P], F32, name="dt%d" % r, tag="GT")
+            hn = cn[:, :, I + P * r : I + P * (r + 1)]
+            for i in range(BT):
+                nc.tensor.matmul(
+                    out=rt[:, i, :], lhsT=lin[:, P * i : P * (i + 1)], rhs=ident_f[:],
+                    is_transpose=True, start=True, stop=False,
+                )
+                nc.tensor.matmul(
+                    out=rt[:, i, :], lhsT=sq[:, P * i : P * (i + 1)], rhs=ident_f[:],
+                    is_transpose=True, start=False, stop=True,
+                )
+            nc.tensor.matmul(out=dt[:], lhsT=ident_b[:], rhs=hn, start=True, stop=False)
+            for i in range(BT):
+                nc.tensor.matmul(
+                    out=dt[:, i, :], lhsT=gn[:, P * i : P * (i + 1)], rhs=ident_f[:],
+                    is_transpose=True, start=False, stop=(i == BT - 1),
+                )
+            dec = epi.tile([P, BT, P], F32, name="dec%d" % r, tag="dec")
+            for i in range(BT):
+                nc.scalar.activation(
+                    out=dec[:, i, :], in_=rt[:, i, :], func=ACT.Exp, scale=cst[:, 64 + i : 65 + i]
+                )
+            nc.vector.scalar_tensor_tensor(
+                out=dec[:], in0=dec[:], scalar=-1.0, in1=dt[:], op0=ALU.add, op1=ALU.mult
+            )
+            nc.vector.tensor_tensor(
+                out=osb[:, :, P * q : P * (q + 1)], in0=dec[:], in1=hn, op=ALU.add
+            )
+
+        out_v = out.rearrange("(i p) c -> p i c", p=P)
+        per_slab = 2 * PASSES
+        n_loaded = 2
+        r = 0
+        kk = 0
+        for s, wd in enumerate(SLABS):
+            first = s * per_slab
+            pw = PIECES[s]
+            for n in range(first, first + per_slab):
+                if n >= n_loaded:
+                    load_chunk(n)
+            osb = epi.tile([P, BT, wd], F32, name="osb%d" % s, tag="osb")
+            c0_ = chunks[first][3]
+            for cpos in range(0, wd, pw):
+                prev = None
+                for n in range(first, first + per_slab):
+                    regroup(n, cpos, pw, kk)
+                    if prev is not None:
+                        quantise(*prev)
+                    prev = (n, cpos, pw, kk)
+                    kk += 1
+                quantise(*prev)
+                for q in range(cpos // P, (cpos + pw) // P):
+                    round_(s, q, r, osb)
+                    r += 1
+            nc.sync.dma_start(out=out_v[:, :, c0_ : c0_ + wd], in_=osb[:])

@@ -23,10 +23,12 @@ EPS = 1e-6
 FLOPS = 2 * 2 * B * K * H
 
 SLABS = (512, 512, 512, 512)
-S_PATTERN = "VSVVSVSVVS"
-PIECES = (512, 512, 512, 128)
-RAW_BUFS = 10
-GRP_BUFS = 4
+RAW_BUFS = 12
+FILL = 4
+QUOTA = (6, 6, 5, 5, 5, 5, 5, 3, 3, 3, 3, 4, 4, 3)
+WQ_BUFS = 9
+GRP_BUFS = 14
+ROUNDS = H // P
 
 
 def tile_ltccell_kernel(
@@ -36,69 +38,66 @@ def tile_ltccell_kernel(
     weights = (W_mod, W_tgt)
     with ExitStack() as ctx:
         const = ctx.enter_context(tc.tile_pool(name="const", bufs=1))
-        rawp = ctx.enter_context(tc.tile_pool(name="rawp", bufs=RAW_BUFS))
+        rawp = ctx.enter_context(tc.tile_pool(name="rawp", bufs=1))
         grpp = ctx.enter_context(tc.tile_pool(name="grpp", bufs=GRP_BUFS))
         cgp = ctx.enter_context(tc.tile_pool(name="cgp", bufs=2))
-        wqp = ctx.enter_context(tc.tile_pool(name="wqp", bufs=2))
+        wqp = ctx.enter_context(tc.tile_pool(name="wqp", bufs=WQ_BUFS))
         epi = ctx.enter_context(tc.tile_pool(name="epi", bufs=2))
         psum = ctx.enter_context(tc.psum_pool(name="psum", bufs=2))
 
         warm = const.tile([P, 1], F32, name="warm")
         nc.vector.memset(warm[:], 0.0)
         nc.scalar.activation(out=warm[:], in_=warm[:], func=ACT.Exp)
-
         vecs = const.tile([P, P], BF16, name="vecs")
         nc.vector.memset(vecs[:], 0.0)
         for v, vec in enumerate((b_mod, b_tgt, log_tau, bias)):
             nc.scalar.dma_start(
-                out=vecs[16 * v : 16 * v + 16, :],
-                in_=vec.rearrange("(r c) -> r c", c=P),
+                out=vecs[16 * v : 16 * v + 16, :], in_=vec.rearrange("(r c) -> r c", c=P)
             )
         nc.scalar.dma_start(
-            out=vecs[64 : 64 + BT, :],
-            in_=time_delta.rearrange("(i c) o -> i (c o)", c=P),
+            out=vecs[64 : 64 + BT, :], in_=time_delta.rearrange("(i c) o -> i (c o)", c=P)
         )
         ident_f = const.tile([P, P], F32, name="ident_f")
         make_identity(nc, ident_f[:])
         ident_b = const.tile([P, P], BF16, name="ident_b")
         make_identity(nc, ident_b[:])
 
+        cn = []
+        for g in range(PASSES):
+            src = x if g == 0 else h[:, K_PASS * (g - 1) : K_PASS * g]
+            cng = const.tile([P, BT, K_PASS], BF16, name="cn%d" % g)
+            nc.sync.dma_start(out=cng[:], in_=src.rearrange("(i p) k -> p i k", p=P))
+            cn.append(cng)
         chunks = []
         col0 = 0
-        for s, wd in enumerate(SLABS):
+        for wd in SLABS:
             for g in range(PASSES):
                 for m in range(2):
-                    chunks.append((s, g, m, col0, wd))
+                    chunks.append((col0, wd, g, m))
             col0 += wd
-
         raws = {}
+        state = {"next": 0, "free": RAW_BUFS}
 
-        def load_chunk(n):
-            s, g, m, c0, wd = chunks[n]
-            raw = rawp.tile([P, PACK, wd], BF16, name="raw%d" % n, tag="raw")
-            nc.sync.dma_start(
-                out=raw[:],
-                in_=weights[m][K_PASS * g : K_PASS * (g + 1), c0 : c0 + wd].rearrange(
-                    "(p j) w -> p j w", j=PACK
-                ),
-            )
-            raws[n] = raw
+        def load_more():
+            while state["next"] < len(chunks) and state["free"] > 0:
+                c0, wd, g, m = chunks[state["next"]]
+                raw = rawp.tile(
+                    [P, PACK, wd], BF16, name="raw%d" % state["next"], tag="raw", bufs=RAW_BUFS,
+                )
+                nc.sync.dma_start(
+                    out=raw[:],
+                    in_=weights[m][K_PASS * g : K_PASS * (g + 1), c0 : c0 + wd].rearrange(
+                        "(p j) w -> p j w", j=PACK
+                    ),
+                )
+                for r in range(c0 // P, (c0 + wd) // P):
+                    raws[(r, g, m)] = (raw, c0, wd)
+                state["free"] -= 1
+                state["next"] += 1
 
-        cn = const.tile([P, BT, K], BF16, name="cn")
+        load_more()
 
-        def load_c(g):
-            src = x if g == 0 else h[:, K_PASS * (g - 1) : K_PASS * g]
-            nc.sync.dma_start(
-                out=cn[:, :, K_PASS * g : K_PASS * (g + 1)],
-                in_=src.rearrange("(i p) k -> p i k", p=P),
-            )
-
-        load_chunk(0)
-        load_chunk(1)
-        for g in range(PASSES):
-            load_c(g)
-
-        pst = psum.tile([P, P], BF16, name="pst", tag="GT")
+        pst = psum.tile([P, P], BF16, name="pst", tag="DT")
         nc.tensor.transpose(pst[:], vecs[:], ident_b[:])
         cst = const.tile([P, P], F32, name="cst")
         nc.vector.tensor_copy(out=cst[:], in_=pst[:])
@@ -118,16 +117,16 @@ def tile_ltccell_kernel(
         nc.vector.scalar_tensor_tensor(
             out=c1[:], in0=nk0[:], scalar=-1.0, in1=nk0[:], op0=ALU.mult, op1=ALU.mult
         )
-        c0 = const.tile([P, 16], F32, name="c0")
-        nc.vector.tensor_tensor(out=c0[:], in0=nk0[:], in1=itau[:], op=ALU.mult)
+        c0t = const.tile([P, 16], F32, name="c0t")
+        nc.vector.tensor_tensor(out=c0t[:], in0=nk0[:], in1=itau[:], op=ALU.mult)
 
-        cnf = cn[:].bitcast(F32).rearrange("p i (g q u) -> p i g u q", g=PASSES, u=2)
         cq = []
         cs = []
-        bank_tags = ("F", "A", "RT", "GT")
+        bank_tags = ("F", "A", "RT", "DT")
         for g in range(PASSES):
             cg = cgp.tile([P, B * PACK], BF16, name="cg%d" % g, tag="cg", align_bytes=64)
             cgf = cg[:].bitcast(F32).rearrange("p (b u) -> p b u", u=2)
+            cnf = cn[g][:].bitcast(F32).rearrange("p i (q u) -> p i u q", u=2)
             for half in range(2):
                 xt = psum.tile(
                     [P, 2, 2, P], F32, name="xt%d_%d" % (g, half), tag=bank_tags[(2 * g + half) % 4]
@@ -135,7 +134,7 @@ def tile_ltccell_kernel(
                 for il in range(2):
                     for u in range(2):
                         nc.tensor.transpose(
-                            xt[:, u, il, :], cnf[:, 2 * half + il, g, u, :], ident_f[:]
+                            xt[:, u, il, :], cnf[:, 2 * half + il, u, :], ident_f[:]
                         )
                 dst = cgf[:, 256 * half : 256 * half + 256, :]
                 src = xt[:].rearrange("p u i b -> p (i b) u")
@@ -151,118 +150,177 @@ def tile_ltccell_kernel(
 
         grps = {}
         wqs = {}
+        t = {}
 
-        def regroup(n, cpos, pw, k):
-            grp = grpp.tile([P, pw, PACK], BF16, name="grp%d" % k, tag="grp", align_bytes=64)
-            dst = grp[:].rearrange("p (c i) t -> p c t i", i=4)
-            src = raws[n][:, :, cpos : cpos + pw].rearrange("p t (c i) -> p c t i", i=4)
-            if S_PATTERN[k % len(S_PATTERN)] == "S":
+        def new_grp(r, g):
+            grps[(r, g)] = grpp.tile(
+                [P, 2, P, PACK], BF16, name="grp%d_%d" % (r, g), tag="grp", align_bytes=64
+            )
+
+        def copy(r, g, m, eng):
+            raw, c0, wd = raws[(r, g, m)]
+            o = P * r - c0
+            dst = grps[(r, g)][:, m, :, :].rearrange("p (c i) t -> p c t i", i=4)
+            src = raw[:, :, o : o + P].rearrange("p t (c i) -> p c t i", i=4)
+            if eng == "S":
                 nc.scalar.copy(out=dst, in_=src)
             else:
                 nc.vector.tensor_copy(out=dst, in_=src)
-            grps[k] = grp
+            if o + P == wd:
+                state["free"] += 1
+                load_more()
 
-        def quantise(n, cpos, pw, k):
-            s, g, m, c0_, wd = chunks[n]
-            wq = wqp.tile([P, pw], U32, name="wq%d" % k, tag="wq%d_%d" % (m, g), align_bytes=64)
-            ws = wqp.tile([P, pw], U8, name="ws%d" % k, tag="ws%d_%d" % (m, g), align_bytes=64)
+        def quantise(r, g):
+            wq = wqp.tile([P, 2 * P], U32, name="wq%d_%d" % (r, g), tag="wq%d" % g, align_bytes=64)
+            ws = wqp.tile([P, 2 * P], U8, name="ws%d_%d" % (r, g), tag="ws%d" % g, align_bytes=64)
             nc.vector.quantize_mx(
-                out=wq[:].bitcast(FP8X4),
-                scales=ws[:],
-                in_=grps[k][:].rearrange("p w t -> p (w t)"),
+                out=wq[:].bitcast(FP8X4), scales=ws[:],
+                in_=grps[(r, g)][:].rearrange("p m w t -> p (m w t)"),
             )
-            wqs[(s, g, m, cpos // pw)] = (wq, ws)
-
-        def round_(s, q, r, osb):
-            acc = []
             for m in range(2):
-                ps = psum.tile([P, B], F32, name="ps%d_%d" % (m, r), tag=("F", "A")[m])
-                for g in range(PASSES):
-                    pw = PIECES[s]
-                    wq, ws = wqs[(s, g, m, P * q // pw)]
-                    o = P * q % pw
-                    nc.tensor.matmul_mx(
-                        out=ps[:],
-                        lhsT=wq[:, o : o + P].bitcast(FP8X4),
-                        lhsT_scale=ws[:, o : o + P],
-                        rhs=cq[g][:].bitcast(FP8X4),
-                        rhs_scale=cs[g][:],
-                        start=(g == 0),
-                        stop=(g == PASSES - 1),
-                    )
-                acc.append(ps)
-            u = epi.tile([P, B], F32, name="u%d" % r, tag="u")
-            nc.scalar.activation(out=u[:], in_=acc[0][:], func=ACT.Abs, bias=cst[:, r : r + 1])
-            nc.scalar.activation(out=u[:], in_=u[:], func=ACT.Tanh)
-            a = epi.tile([P, B], F32, name="a%d" % r, tag="a")
-            nc.scalar.activation(
-                out=a[:], in_=acc[1][:], func=ACT.Tanh, bias=cst[:, 16 + r : 17 + r]
+                wqs[(r, g, m)] = (wq, ws, m * P)
+
+        def mx_pass(r, m, g):
+            if g == 0:
+                t[("ps", r, m)] = psum.tile([P, B], F32, name="ps%d_%d" % (m, r), tag=("F", "A")[m])
+            wq, ws, o = wqs[(r, g, m)]
+            nc.tensor.matmul_mx(
+                out=t[("ps", r, m)][:],
+                lhsT=wq[:, o : o + P].bitcast(FP8X4), lhsT_scale=ws[:, o : o + P],
+                rhs=cq[g][:].bitcast(FP8X4), rhs_scale=cs[g][:],
+                start=(g == 0), stop=(g == PASSES - 1),
             )
+
+        def s_front(r):
+            a = epi.tile([P, B], F32, name="a%d" % r, tag="a")
+            nc.scalar.activation(out=a[:], in_=t[("ps", r, 1)][:], func=ACT.Tanh, bias=cst[:, 16 + r : 17 + r])
+            u = epi.tile([P, B], F32, name="u%d" % r, tag="u")
+            nc.scalar.activation(out=u[:], in_=t[("ps", r, 0)][:], func=ACT.Abs, bias=cst[:, r : r + 1])
+            nc.scalar.activation(out=u[:], in_=u[:], func=ACT.Tanh)
             sq = epi.tile([P, B], F32, name="sq%d" % r, tag="sq")
             nc.scalar.activation(out=sq[:], in_=u[:], func=ACT.Square, scale=sqe[:, r : r + 1])
-            lin = epi.tile([P, B], F32, name="lin%d" % r, tag="lin")
-            nc.vector.tensor_scalar(
-                out=lin[:], in0=u[:], scalar1=c1[:, r : r + 1], scalar2=c0[:, r : r + 1],
-                op0=ALU.mult, op1=ALU.add,
-            )
+            t[("a", r)] = a
+            t[("u", r)] = u
+            t[("sq", r)] = sq
+
+        def v_gn(r):
             gn = epi.tile([P, B], F32, name="gn%d" % r, tag="gn")
             nc.vector.tensor_scalar(
-                out=gn[:], in0=a[:], scalar1=cst[:, 48 + r : 49 + r], scalar2=-1.0,
+                out=gn[:], in0=t[("a", r)][:], scalar1=cst[:, 48 + r : 49 + r], scalar2=-1.0,
                 op0=ALU.add, op1=ALU.mult,
             )
+            t[("gn", r)] = gn
+
+        def v_lin(r):
+            lin = epi.tile([P, B], F32, name="lin%d" % r, tag="lin")
+            nc.vector.tensor_scalar(
+                out=lin[:], in0=t[("u", r)][:], scalar1=c1[:, r : r + 1], scalar2=c0t[:, r : r + 1],
+                op0=ALU.mult, op1=ALU.add,
+            )
+            t[("lin", r)] = lin
+
+        def hn(r):
+            return cn[1 + r // 4][:, :, P * (r % 4) : P * (r % 4 + 1)]
+
+        def pe_back(r):
+            dt = psum.tile([P, BT, P], F32, name="dt%d" % r, tag="DT")
             rt = psum.tile([P, BT, P], F32, name="rt%d" % r, tag="RT")
-            dt = psum.tile([P, BT, P], F32, name="dt%d" % r, tag="GT")
-            hn = cn[:, :, I + P * r : I + P * (r + 1)]
             for i in range(BT):
                 nc.tensor.matmul(
-                    out=rt[:, i, :], lhsT=lin[:, P * i : P * (i + 1)], rhs=ident_f[:],
+                    out=rt[:, i, :], lhsT=t[("lin", r)][:, P * i : P * (i + 1)], rhs=ident_f[:],
                     is_transpose=True, start=True, stop=False,
                 )
                 nc.tensor.matmul(
-                    out=rt[:, i, :], lhsT=sq[:, P * i : P * (i + 1)], rhs=ident_f[:],
+                    out=rt[:, i, :], lhsT=t[("sq", r)][:, P * i : P * (i + 1)], rhs=ident_f[:],
                     is_transpose=True, start=False, stop=True,
                 )
-            nc.tensor.matmul(out=dt[:], lhsT=ident_b[:], rhs=hn, start=True, stop=False)
+            nc.tensor.matmul(out=dt[:], lhsT=ident_b[:], rhs=hn(r), start=True, stop=False)
             for i in range(BT):
                 nc.tensor.matmul(
-                    out=dt[:, i, :], lhsT=gn[:, P * i : P * (i + 1)], rhs=ident_f[:],
+                    out=dt[:, i, :], lhsT=t[("gn", r)][:, P * i : P * (i + 1)], rhs=ident_f[:],
                     is_transpose=True, start=False, stop=(i == BT - 1),
                 )
+            t[("rt", r)] = rt
+            t[("dt", r)] = dt
+
+        def s_exp(r):
             dec = epi.tile([P, BT, P], F32, name="dec%d" % r, tag="dec")
             for i in range(BT):
                 nc.scalar.activation(
-                    out=dec[:, i, :], in_=rt[:, i, :], func=ACT.Exp, scale=cst[:, 64 + i : 65 + i]
+                    out=dec[:, i, :], in_=t[("rt", r)][:, i, :], func=ACT.Exp, scale=cst[:, 64 + i : 65 + i]
                 )
-            nc.vector.scalar_tensor_tensor(
-                out=dec[:], in0=dec[:], scalar=-1.0, in1=dt[:], op0=ALU.add, op1=ALU.mult
-            )
-            nc.vector.tensor_tensor(
-                out=osb[:, :, P * q : P * (q + 1)], in0=dec[:], in1=hn, op=ALU.add
-            )
+            t[("dec", r)] = dec
 
         out_v = out.rearrange("(i p) c -> p i c", p=P)
-        per_slab = 2 * PASSES
-        n_loaded = 2
-        r = 0
-        kk = 0
-        for s, wd in enumerate(SLABS):
-            first = s * per_slab
-            pw = PIECES[s]
-            for n in range(first, first + per_slab):
-                if n >= n_loaded:
-                    load_chunk(n)
-            osb = epi.tile([P, BT, wd], F32, name="osb%d" % s, tag="osb")
-            c0_ = chunks[first][3]
-            for cpos in range(0, wd, pw):
-                prev = None
-                for n in range(first, first + per_slab):
-                    regroup(n, cpos, pw, kk)
-                    if prev is not None:
-                        quantise(*prev)
-                    prev = (n, cpos, pw, kk)
-                    kk += 1
-                quantise(*prev)
-                for q in range(cpos // P, (cpos + pw) // P):
-                    round_(s, q, r, osb)
-                    r += 1
-            nc.sync.dma_start(out=out_v[:, :, c0_ : c0_ + wd], in_=osb[:])
+
+        def v_blend(r):
+            if r % 2 == 0:
+                t["osb"] = epi.tile([P, BT, 2 * P], F32, name="osb%d" % r, tag="osb", bufs=3)
+            dec = t[("dec", r)]
+            nc.vector.scalar_tensor_tensor(
+                out=dec[:], in0=dec[:], scalar=-1.0, in1=t[("dt", r)][:], op0=ALU.add, op1=ALU.mult
+            )
+            q = r % 2
+            nc.vector.tensor_tensor(
+                out=t["osb"][:, :, P * q : P * (q + 1)], in0=dec[:], in1=hn(r), op=ALU.add
+            )
+            if q == 1:
+                nc.sync.dma_start(out=out_v[:, :, P * (r - 1) : P * (r + 1)], in_=t["osb"][:])
+
+        def by_scalar(r, g):
+            return g < PASSES - 1 and (g > 0 or r % 2 == 1)
+
+        def s_prep(units):
+            for r, g in units:
+                new_grp(r, g)
+                if by_scalar(r, g):
+                    copy(r, g, 1, "S")
+
+        def v_prep(units):
+            for r, g in units:
+                copy(r, g, 0, "V")
+                if not by_scalar(r, g):
+                    copy(r, g, 1, "V")
+            for r, g in units:
+                quantise(r, g)
+
+        for g in range(PASSES):
+            for r in range(FILL):
+                new_grp(r, g)
+                copy(r, g, 1, "S")
+                copy(r, g, 0, "V")
+            for r in range(FILL):
+                quantise(r, g)
+            for r in range(2):
+                for m in range(2):
+                    mx_pass(r, m, g)
+        stream = [(r, g) for s in (1, 2) for g in range(PASSES) for r in range(4 * s, 4 * s + 4)]
+        stream += [(r, g) for r in range(12, ROUNDS) for g in range(PASSES)]
+        sets = []
+        pos = 0
+        for n in QUOTA:
+            sets.append(stream[pos : pos + n])
+            pos += n
+        assert pos == len(stream)
+        s_prep(sets[0])
+
+        for j in range(ROUNDS + 1):
+            if j >= 1:
+                pe_back(j - 1)
+            if 2 <= j + 1 < ROUNDS:
+                for m in (1, 0):
+                    for g in range(PASSES):
+                        mx_pass(j + 1, m, g)
+            if j < ROUNDS:
+                s_front(j)
+            if j >= 1:
+                s_exp(j - 1)
+            if j + 1 < len(sets):
+                s_prep(sets[j + 1])
+            if j < len(sets):
+                v_prep(sets[j])
+            if j < ROUNDS:
+                v_gn(j)
+                v_lin(j)
+            if j >= 1:
+                v_blend(j - 1)

@@ -23,12 +23,12 @@ EPS = 1e-6
 FLOPS = 2 * 2 * B * K * H
 
 SLABS = (512, 512, 512, 512)
-RAW_BUFS = 12
-FILL = 4
-QUOTA = (6, 6, 5, 5, 5, 5, 5, 3, 3, 3, 3, 4, 4, 3)
-WQ_BUFS = 9
-GRP_BUFS = 14
+RAW_BUFS = 18
+SPANS = ((0, 2), (2, 2), (4, 2), (6, 2), (8, 2), (10, 2), (12, 2), (14, 1), (15, 1))
+GRP_BUFS = {2: 4, 1: 4}
+WQ_BUFS = {2: 3, 1: 2}
 ROUNDS = H // P
+S_UNITS = tuple((sp, g) for sp in range(len(SPANS)) for g in range(5) if (g < 4 and (g > 0 or sp % 2 == 1)))
 
 
 def tile_ltccell_kernel(
@@ -39,9 +39,9 @@ def tile_ltccell_kernel(
     with ExitStack() as ctx:
         const = ctx.enter_context(tc.tile_pool(name="const", bufs=1))
         rawp = ctx.enter_context(tc.tile_pool(name="rawp", bufs=1))
-        grpp = ctx.enter_context(tc.tile_pool(name="grpp", bufs=GRP_BUFS))
+        grpp = ctx.enter_context(tc.tile_pool(name="grpp", bufs=1))
         cgp = ctx.enter_context(tc.tile_pool(name="cgp", bufs=2))
-        wqp = ctx.enter_context(tc.tile_pool(name="wqp", bufs=WQ_BUFS))
+        wqp = ctx.enter_context(tc.tile_pool(name="wqp", bufs=1))
         epi = ctx.enter_context(tc.tile_pool(name="epi", bufs=2))
         psum = ctx.enter_context(tc.psum_pool(name="psum", bufs=2))
 
@@ -57,6 +57,12 @@ def tile_ltccell_kernel(
         nc.scalar.dma_start(
             out=vecs[64 : 64 + BT, :], in_=time_delta.rearrange("(i c) o -> i (c o)", c=P)
         )
+        brow = const.tile([P, H], BF16, name="brow")
+        nc.vector.memset(brow[:], 0.0)
+        nc.scalar.dma_start(out=brow[0:1, :], in_=bias.rearrange("(o c) -> o c", o=1))
+        neg0 = const.tile([P, P], BF16, name="neg0")
+        nc.vector.memset(neg0[:], 0.0)
+        nc.vector.memset(neg0[0:1, :], -1.0)
         ident_f = const.tile([P, P], F32, name="ident_f")
         make_identity(nc, ident_f[:])
         ident_b = const.tile([P, P], BF16, name="ident_b")
@@ -117,6 +123,8 @@ def tile_ltccell_kernel(
         nc.vector.scalar_tensor_tensor(
             out=c1[:], in0=nk0[:], scalar=-1.0, in1=nk0[:], op0=ALU.mult, op1=ALU.mult
         )
+        nbt = const.tile([P, 16], F32, name="nbt")
+        nc.vector.tensor_scalar(out=nbt[:], in0=cst[:, 16:32], scalar1=-1.0, scalar2=None, op0=ALU.mult)
         c0t = const.tile([P, 16], F32, name="c0t")
         nc.vector.tensor_tensor(out=c0t[:], in0=nk0[:], in1=itau[:], op=ALU.mult)
 
@@ -152,33 +160,40 @@ def tile_ltccell_kernel(
         wqs = {}
         t = {}
 
-        def new_grp(r, g):
-            grps[(r, g)] = grpp.tile(
-                [P, 2, P, PACK], BF16, name="grp%d_%d" % (r, g), tag="grp", align_bytes=64
+        def new_grp(sp, g):
+            r0, nr = SPANS[sp]
+            grps[(sp, g)] = grpp.tile(
+                [P, 2, nr * P, PACK], BF16, name="grp%d_%d" % (sp, g), tag="grp%d" % nr,
+                align_bytes=64, bufs=GRP_BUFS[nr],
             )
 
-        def copy(r, g, m, eng):
-            raw, c0, wd = raws[(r, g, m)]
-            o = P * r - c0
-            dst = grps[(r, g)][:, m, :, :].rearrange("p (c i) t -> p c t i", i=4)
-            src = raw[:, :, o : o + P].rearrange("p t (c i) -> p c t i", i=4)
+        def copy(sp, g, m, eng):
+            r0, nr = SPANS[sp]
+            raw, c0, wd = raws[(r0, g, m)]
+            o = P * r0 - c0
+            dst = grps[(sp, g)][:, m, :, :].rearrange("p (c i) t -> p c t i", i=4)
+            src = raw[:, :, o : o + nr * P].rearrange("p t (c i) -> p c t i", i=4)
             if eng == "S":
                 nc.scalar.copy(out=dst, in_=src)
             else:
                 nc.vector.tensor_copy(out=dst, in_=src)
-            if o + P == wd:
+            if o + nr * P == wd:
                 state["free"] += 1
                 load_more()
 
-        def quantise(r, g):
-            wq = wqp.tile([P, 2 * P], U32, name="wq%d_%d" % (r, g), tag="wq%d" % g, align_bytes=64)
-            ws = wqp.tile([P, 2 * P], U8, name="ws%d_%d" % (r, g), tag="ws%d" % g, align_bytes=64)
+        def quantise(sp, g):
+            r0, nr = SPANS[sp]
+            wq = wqp.tile([P, 2 * nr * P], U32, name="wq%d_%d" % (sp, g), tag="wq%d_%d" % (nr, g),
+                          align_bytes=64, bufs=WQ_BUFS[nr])
+            ws = wqp.tile([P, 2 * nr * P], U8, name="ws%d_%d" % (sp, g), tag="ws%d_%d" % (nr, g),
+                          align_bytes=64, bufs=WQ_BUFS[nr])
             nc.vector.quantize_mx(
                 out=wq[:].bitcast(FP8X4), scales=ws[:],
-                in_=grps[(r, g)][:].rearrange("p m w t -> p (m w t)"),
+                in_=grps[(sp, g)][:].rearrange("p m w t -> p (m w t)"),
             )
-            for m in range(2):
-                wqs[(r, g, m)] = (wq, ws, m * P)
+            for r in range(r0, r0 + nr):
+                for m in range(2):
+                    wqs[(r, g, m)] = (wq, ws, (m * nr + r - r0) * P)
 
         def mx_pass(r, m, g):
             if g == 0:
@@ -193,7 +208,7 @@ def tile_ltccell_kernel(
 
         def s_front(r):
             a = epi.tile([P, B], F32, name="a%d" % r, tag="a")
-            nc.scalar.activation(out=a[:], in_=t[("ps", r, 1)][:], func=ACT.Tanh, bias=cst[:, 16 + r : 17 + r])
+            nc.scalar.activation(out=a[:], in_=t[("ps", r, 1)][:], func=ACT.Tanh, bias=nbt[:, r : r + 1], scale=-1.0)
             u = epi.tile([P, B], F32, name="u%d" % r, tag="u")
             nc.scalar.activation(out=u[:], in_=t[("ps", r, 0)][:], func=ACT.Abs, bias=cst[:, r : r + 1])
             nc.scalar.activation(out=u[:], in_=u[:], func=ACT.Tanh)
@@ -202,14 +217,6 @@ def tile_ltccell_kernel(
             t[("a", r)] = a
             t[("u", r)] = u
             t[("sq", r)] = sq
-
-        def v_gn(r):
-            gn = epi.tile([P, B], F32, name="gn%d" % r, tag="gn")
-            nc.vector.tensor_scalar(
-                out=gn[:], in0=t[("a", r)][:], scalar1=cst[:, 48 + r : 49 + r], scalar2=-1.0,
-                op0=ALU.add, op1=ALU.mult,
-            )
-            t[("gn", r)] = gn
 
         def v_lin(r):
             lin = epi.tile([P, B], F32, name="lin%d" % r, tag="lin")
@@ -235,9 +242,14 @@ def tile_ltccell_kernel(
                     is_transpose=True, start=False, stop=True,
                 )
             nc.tensor.matmul(out=dt[:], lhsT=ident_b[:], rhs=hn(r), start=True, stop=False)
+            nc.tensor.matmul(
+                out=dt[:], lhsT=neg0[:],
+                rhs=brow[:, P * r : P * (r + 1)].unsqueeze(1).to_broadcast([P, BT, P]),
+                start=False, stop=False,
+            )
             for i in range(BT):
                 nc.tensor.matmul(
-                    out=dt[:, i, :], lhsT=t[("gn", r)][:, P * i : P * (i + 1)], rhs=ident_f[:],
+                    out=dt[:, i, :], lhsT=t[("a", r)][:, P * i : P * (i + 1)], rhs=ident_f[:],
                     is_transpose=True, start=False, stop=(i == BT - 1),
                 )
             t[("rt", r)] = rt
@@ -267,40 +279,40 @@ def tile_ltccell_kernel(
             if q == 1:
                 nc.sync.dma_start(out=out_v[:, :, P * (r - 1) : P * (r + 1)], in_=t["osb"][:])
 
-        def by_scalar(r, g):
-            return g < PASSES - 1 and (g > 0 or r % 2 == 1)
+        def by_scalar(sp, g):
+            return (sp, g) in S_UNITS
 
         def s_prep(units):
-            for r, g in units:
-                new_grp(r, g)
-                if by_scalar(r, g):
-                    copy(r, g, 1, "S")
+            for sp, g in units:
+                new_grp(sp, g)
+                if by_scalar(sp, g):
+                    copy(sp, g, 1, "S")
 
         def v_prep(units):
-            for r, g in units:
-                copy(r, g, 0, "V")
-                if not by_scalar(r, g):
-                    copy(r, g, 1, "V")
-            for r, g in units:
-                quantise(r, g)
+            for sp, g in units:
+                copy(sp, g, 0, "V")
+                if not by_scalar(sp, g):
+                    copy(sp, g, 1, "V")
+            for sp, g in units:
+                quantise(sp, g)
 
         for g in range(PASSES):
-            for r in range(FILL):
-                new_grp(r, g)
-                copy(r, g, 1, "S")
-                copy(r, g, 0, "V")
-            for r in range(FILL):
-                quantise(r, g)
+            s_prep([(0, g)])
+            v_prep([(0, g)])
             for r in range(2):
                 for m in range(2):
                     mx_pass(r, m, g)
-        stream = [(r, g) for s in (1, 2) for g in range(PASSES) for r in range(4 * s, 4 * s + 4)]
-        stream += [(r, g) for r in range(12, ROUNDS) for g in range(PASSES)]
-        sets = []
+        stream = [(sp, g) for sp in range(1, len(SPANS)) for g in range(PASSES)]
+        sets = [[] for j in range(ROUNDS - 2)]
         pos = 0
-        for n in QUOTA:
-            sets.append(stream[pos : pos + n])
-            pos += n
+        total = sum(SPANS[sp][1] for sp, g in stream)
+        done = 0
+        for j in range(ROUNDS - 2):
+            target = total * (j + 1) / (ROUNDS - 2)
+            while pos < len(stream) and (done < target or SPANS[stream[pos][0]][0] <= j + 2):
+                sets[j].append(stream[pos])
+                done += SPANS[stream[pos][0]][1]
+                pos += 1
         assert pos == len(stream)
         s_prep(sets[0])
 
@@ -320,7 +332,6 @@ def tile_ltccell_kernel(
             if j < len(sets):
                 v_prep(sets[j])
             if j < ROUNDS:
-                v_gn(j)
                 v_lin(j)
             if j >= 1:
                 v_blend(j - 1)

@@ -28,7 +28,7 @@ SPANS = ((0, 2), (2, 2), (4, 2), (6, 2), (8, 2), (10, 2), (12, 2), (14, 1), (15,
 GRP_BUFS = {2: 4, 1: 4}
 WQ_BUFS = {2: 3, 1: 2}
 ROUNDS = H // P
-S_UNITS = tuple((sp, g) for sp in range(len(SPANS)) for g in range(5) if (g < 4 and (g > 0 or sp % 2 == 1)))
+S_UNITS = tuple((sp, g) for sp in range(len(SPANS)) for g in range(5) if g in (1, 3))
 
 
 def tile_ltccell_kernel(

@@ -22,13 +22,15 @@ BT = B // P
 EPS = 1e-6
 FLOPS = 2 * 2 * B * K * H
 
-SLABS = (512, 512, 512, 512)
+SLABS = (256, 256, 256, 256, 512, 512)
 RAW_BUFS = 18
 SPANS = ((0, 2), (2, 2), (4, 2), (6, 2), (8, 2), (10, 2), (12, 2), (14, 1), (15, 1))
 GRP_BUFS = {2: 4, 1: 4}
 WQ_BUFS = {2: 3, 1: 2}
 ROUNDS = H // P
-S_UNITS = tuple((sp, g) for sp in range(len(SPANS)) for g in range(5) if g in (1, 3))
+LATE_G = 10
+LATE_R = 10
+S_UNITS = tuple((sp, g) for sp in range(len(SPANS)) for g in range(5) if (g < 4 and (g > 0 or sp % 2 == 1 or sp >= 4)))
 
 
 def tile_ltccell_kernel(
@@ -125,6 +127,8 @@ def tile_ltccell_kernel(
         )
         nbt = const.tile([P, 16], F32, name="nbt")
         nc.vector.tensor_scalar(out=nbt[:], in0=cst[:, 16:32], scalar1=-1.0, scalar2=None, op0=ALU.mult)
+        k1 = const.tile([P, 16], F32, name="k1")
+        nc.vector.tensor_tensor(out=k1[:], in0=sqe[:], in1=sqe[:], op=ALU.mult)
         c0t = const.tile([P, 16], F32, name="c0t")
         nc.vector.tensor_tensor(out=c0t[:], in0=nk0[:], in1=itau[:], op=ALU.mult)
 
@@ -212,19 +216,35 @@ def tile_ltccell_kernel(
             u = epi.tile([P, B], F32, name="u%d" % r, tag="u")
             nc.scalar.activation(out=u[:], in_=t[("ps", r, 0)][:], func=ACT.Abs, bias=cst[:, r : r + 1])
             nc.scalar.activation(out=u[:], in_=u[:], func=ACT.Tanh)
-            sq = epi.tile([P, B], F32, name="sq%d" % r, tag="sq")
-            nc.scalar.activation(out=sq[:], in_=u[:], func=ACT.Square, scale=sqe[:, r : r + 1])
             t[("a", r)] = a
             t[("u", r)] = u
-            t[("sq", r)] = sq
+            if r < LATE_R:
+                sq = epi.tile([P, B], F32, name="sq%d" % r, tag="sq")
+                nc.scalar.activation(out=sq[:], in_=u[:], func=ACT.Square, scale=sqe[:, r : r + 1])
+                t[("sq", r)] = sq
 
         def v_lin(r):
             lin = epi.tile([P, B], F32, name="lin%d" % r, tag="lin")
-            nc.vector.tensor_scalar(
-                out=lin[:], in0=t[("u", r)][:], scalar1=c1[:, r : r + 1], scalar2=c0t[:, r : r + 1],
-                op0=ALU.mult, op1=ALU.add,
-            )
+            if r < LATE_R:
+                nc.vector.tensor_scalar(
+                    out=lin[:], in0=t[("u", r)][:], scalar1=c1[:, r : r + 1], scalar2=c0t[:, r : r + 1],
+                    op0=ALU.mult, op1=ALU.add,
+                )
+            else:
+                nc.vector.tensor_scalar(
+                    out=lin[:], in0=t[("u", r)][:], scalar1=k1[:, r : r + 1], scalar2=nk0[:, r : r + 1],
+                    op0=ALU.mult, op1=ALU.add,
+                )
+                nc.vector.scalar_tensor_tensor(
+                    out=lin[:], in0=t[("u", r)][:], scalar=itau[:, r : r + 1], in1=lin[:],
+                    op0=ALU.add, op1=ALU.mult,
+                )
             t[("lin", r)] = lin
+            if r >= LATE_G:
+                a = t[("a", r)]
+                nc.vector.tensor_scalar(
+                    out=a[:], in0=a[:], scalar1=cst[:, 48 + r : 49 + r], scalar2=None, op0=ALU.subtract
+                )
 
         def hn(r):
             return cn[1 + r // 4][:, :, P * (r % 4) : P * (r % 4 + 1)]
@@ -235,18 +255,20 @@ def tile_ltccell_kernel(
             for i in range(BT):
                 nc.tensor.matmul(
                     out=rt[:, i, :], lhsT=t[("lin", r)][:, P * i : P * (i + 1)], rhs=ident_f[:],
-                    is_transpose=True, start=True, stop=False,
+                    is_transpose=True, start=True, stop=(r >= LATE_R),
                 )
-                nc.tensor.matmul(
-                    out=rt[:, i, :], lhsT=t[("sq", r)][:, P * i : P * (i + 1)], rhs=ident_f[:],
-                    is_transpose=True, start=False, stop=True,
-                )
+                if r < LATE_R:
+                    nc.tensor.matmul(
+                        out=rt[:, i, :], lhsT=t[("sq", r)][:, P * i : P * (i + 1)], rhs=ident_f[:],
+                        is_transpose=True, start=False, stop=True,
+                    )
             nc.tensor.matmul(out=dt[:], lhsT=ident_b[:], rhs=hn(r), start=True, stop=False)
-            nc.tensor.matmul(
-                out=dt[:], lhsT=neg0[:],
-                rhs=brow[:, P * r : P * (r + 1)].unsqueeze(1).to_broadcast([P, BT, P]),
-                start=False, stop=False,
-            )
+            if r < LATE_G:
+                nc.tensor.matmul(
+                    out=dt[:], lhsT=neg0[:],
+                    rhs=brow[:, P * r : P * (r + 1)].unsqueeze(1).to_broadcast([P, BT, P]),
+                    start=False, stop=False,
+                )
             for i in range(BT):
                 nc.tensor.matmul(
                     out=dt[:, i, :], lhsT=t[("a", r)][:, P * i : P * (i + 1)], rhs=ident_f[:],

@@ -19,18 +19,20 @@ PACK = 4
 K_PASS = P * PACK
 PASSES = K // K_PASS
 BT = B // P
+ROUNDS = H // P
 EPS = 1e-6
 FLOPS = 2 * 2 * B * K * H
 
-SLABS = (256, 256, 256, 256, 512, 512)
+SLAB = 512
 RAW_BUFS = 18
-SPANS = ((0, 2), (2, 2), (4, 2), (6, 2), (8, 2), (10, 2), (12, 2), (14, 1), (15, 1))
+SPANS = tuple((r, 2) for r in range(0, ROUNDS - 2, 2)) + ((ROUNDS - 2, 1), (ROUNDS - 1, 1))
 GRP_BUFS = {2: 4, 1: 4}
 WQ_BUFS = {2: 3, 1: 2}
-ROUNDS = H // P
-LATE_G = 10
-LATE_R = 10
-S_UNITS = tuple((sp, g) for sp in range(len(SPANS)) for g in range(5) if (g < 4 and (g > 0 or sp % 2 == 1 or sp >= 4)))
+LATE = 10
+
+
+def by_scalar(sp, g):
+    return g < PASSES - 1 and (g > 0 or sp % 2 == 1)
 
 
 def tile_ltccell_kernel(
@@ -76,32 +78,28 @@ def tile_ltccell_kernel(
             cng = const.tile([P, BT, K_PASS], BF16, name="cn%d" % g)
             nc.sync.dma_start(out=cng[:], in_=src.rearrange("(i p) k -> p i k", p=P))
             cn.append(cng)
-        chunks = []
-        col0 = 0
-        for wd in SLABS:
-            for g in range(PASSES):
-                for m in range(2):
-                    chunks.append((col0, wd, g, m))
-            col0 += wd
+        chunks = [
+            (c0, g, m) for c0 in range(0, H, SLAB) for g in range(PASSES) for m in range(2)
+        ]
         raws = {}
-        state = {"next": 0, "free": RAW_BUFS}
+        ring = {"next": 0, "free": RAW_BUFS}
 
         def load_more():
-            while state["next"] < len(chunks) and state["free"] > 0:
-                c0, wd, g, m = chunks[state["next"]]
+            while ring["next"] < len(chunks) and ring["free"] > 0:
+                c0, g, m = chunks[ring["next"]]
                 raw = rawp.tile(
-                    [P, PACK, wd], BF16, name="raw%d" % state["next"], tag="raw", bufs=RAW_BUFS,
+                    [P, PACK, SLAB], BF16, name="raw%d" % ring["next"], tag="raw", bufs=RAW_BUFS
                 )
                 nc.sync.dma_start(
                     out=raw[:],
-                    in_=weights[m][K_PASS * g : K_PASS * (g + 1), c0 : c0 + wd].rearrange(
+                    in_=weights[m][K_PASS * g : K_PASS * (g + 1), c0 : c0 + SLAB].rearrange(
                         "(p j) w -> p j w", j=PACK
                     ),
                 )
-                for r in range(c0 // P, (c0 + wd) // P):
-                    raws[(r, g, m)] = (raw, c0, wd)
-                state["free"] -= 1
-                state["next"] += 1
+                for r in range(c0 // P, (c0 + SLAB) // P):
+                    raws[(r, g, m)] = (raw, c0)
+                ring["free"] -= 1
+                ring["next"] += 1
 
         load_more()
 
@@ -126,7 +124,9 @@ def tile_ltccell_kernel(
             out=c1[:], in0=nk0[:], scalar=-1.0, in1=nk0[:], op0=ALU.mult, op1=ALU.mult
         )
         nbt = const.tile([P, 16], F32, name="nbt")
-        nc.vector.tensor_scalar(out=nbt[:], in0=cst[:, 16:32], scalar1=-1.0, scalar2=None, op0=ALU.mult)
+        nc.vector.tensor_scalar(
+            out=nbt[:], in0=cst[:, 16:32], scalar1=-1.0, scalar2=None, op0=ALU.mult
+        )
         k1 = const.tile([P, 16], F32, name="k1")
         nc.vector.tensor_tensor(out=k1[:], in0=sqe[:], in1=sqe[:], op=ALU.mult)
         c0t = const.tile([P, 16], F32, name="c0t")
@@ -162,35 +162,37 @@ def tile_ltccell_kernel(
 
         grps = {}
         wqs = {}
-        t = {}
+        live = {}
 
         def new_grp(sp, g):
-            r0, nr = SPANS[sp]
+            nr = SPANS[sp][1]
             grps[(sp, g)] = grpp.tile(
                 [P, 2, nr * P, PACK], BF16, name="grp%d_%d" % (sp, g), tag="grp%d" % nr,
                 align_bytes=64, bufs=GRP_BUFS[nr],
             )
 
-        def copy(sp, g, m, eng):
+        def regroup(sp, g, m, engine_copy):
             r0, nr = SPANS[sp]
-            raw, c0, wd = raws[(r0, g, m)]
+            raw, c0 = raws[(r0, g, m)]
             o = P * r0 - c0
-            dst = grps[(sp, g)][:, m, :, :].rearrange("p (c i) t -> p c t i", i=4)
-            src = raw[:, :, o : o + nr * P].rearrange("p t (c i) -> p c t i", i=4)
-            if eng == "S":
-                nc.scalar.copy(out=dst, in_=src)
-            else:
-                nc.vector.tensor_copy(out=dst, in_=src)
-            if o + nr * P == wd:
-                state["free"] += 1
+            engine_copy(
+                out=grps[(sp, g)][:, m, :, :].rearrange("p (c i) t -> p c t i", i=4),
+                in_=raw[:, :, o : o + nr * P].rearrange("p t (c i) -> p c t i", i=4),
+            )
+            if o + nr * P == SLAB:
+                ring["free"] += 1
                 load_more()
 
         def quantise(sp, g):
             r0, nr = SPANS[sp]
-            wq = wqp.tile([P, 2 * nr * P], U32, name="wq%d_%d" % (sp, g), tag="wq%d_%d" % (nr, g),
-                          align_bytes=64, bufs=WQ_BUFS[nr])
-            ws = wqp.tile([P, 2 * nr * P], U8, name="ws%d_%d" % (sp, g), tag="ws%d_%d" % (nr, g),
-                          align_bytes=64, bufs=WQ_BUFS[nr])
+            wq = wqp.tile(
+                [P, 2 * nr * P], U32, name="wq%d_%d" % (sp, g), tag="wq%d_%d" % (nr, g),
+                align_bytes=64, bufs=WQ_BUFS[nr],
+            )
+            ws = wqp.tile(
+                [P, 2 * nr * P], U8, name="ws%d_%d" % (sp, g), tag="ws%d_%d" % (nr, g),
+                align_bytes=64, bufs=WQ_BUFS[nr],
+            )
             nc.vector.quantize_mx(
                 out=wq[:].bitcast(FP8X4), scales=ws[:],
                 in_=grps[(sp, g)][:].rearrange("p m w t -> p (m w t)"),
@@ -199,71 +201,94 @@ def tile_ltccell_kernel(
                 for m in range(2):
                     wqs[(r, g, m)] = (wq, ws, (m * nr + r - r0) * P)
 
+        def scalar_prep(units):
+            for sp, g in units:
+                new_grp(sp, g)
+                if by_scalar(sp, g):
+                    regroup(sp, g, 1, nc.scalar.copy)
+
+        def vector_prep(units):
+            for sp, g in units:
+                regroup(sp, g, 0, nc.vector.tensor_copy)
+                if not by_scalar(sp, g):
+                    regroup(sp, g, 1, nc.vector.tensor_copy)
+            for sp, g in units:
+                quantise(sp, g)
+
         def mx_pass(r, m, g):
             if g == 0:
-                t[("ps", r, m)] = psum.tile([P, B], F32, name="ps%d_%d" % (m, r), tag=("F", "A")[m])
+                live[("z", r, m)] = psum.tile(
+                    [P, B], F32, name="ps%d_%d" % (m, r), tag=("F", "A")[m]
+                )
             wq, ws, o = wqs[(r, g, m)]
             nc.tensor.matmul_mx(
-                out=t[("ps", r, m)][:],
+                out=live[("z", r, m)][:],
                 lhsT=wq[:, o : o + P].bitcast(FP8X4), lhsT_scale=ws[:, o : o + P],
                 rhs=cq[g][:].bitcast(FP8X4), rhs_scale=cs[g][:],
                 start=(g == 0), stop=(g == PASSES - 1),
             )
 
-        def s_front(r):
+        def scalar_front(r):
             a = epi.tile([P, B], F32, name="a%d" % r, tag="a")
-            nc.scalar.activation(out=a[:], in_=t[("ps", r, 1)][:], func=ACT.Tanh, bias=nbt[:, r : r + 1], scale=-1.0)
+            nc.scalar.activation(
+                out=a[:], in_=live[("z", r, 1)][:], func=ACT.Tanh, bias=nbt[:, r : r + 1], scale=-1.0
+            )
             u = epi.tile([P, B], F32, name="u%d" % r, tag="u")
-            nc.scalar.activation(out=u[:], in_=t[("ps", r, 0)][:], func=ACT.Abs, bias=cst[:, r : r + 1])
+            nc.scalar.activation(
+                out=u[:], in_=live[("z", r, 0)][:], func=ACT.Abs, bias=cst[:, r : r + 1]
+            )
             nc.scalar.activation(out=u[:], in_=u[:], func=ACT.Tanh)
-            t[("a", r)] = a
-            t[("u", r)] = u
-            if r < LATE_R:
+            live[("a", r)] = a
+            live[("u", r)] = u
+            if r < LATE:
                 sq = epi.tile([P, B], F32, name="sq%d" % r, tag="sq")
                 nc.scalar.activation(out=sq[:], in_=u[:], func=ACT.Square, scale=sqe[:, r : r + 1])
-                t[("sq", r)] = sq
+                live[("sq", r)] = sq
 
-        def v_lin(r):
+        def vector_front(r):
             lin = epi.tile([P, B], F32, name="lin%d" % r, tag="lin")
-            if r < LATE_R:
+            u = live[("u", r)]
+            if r < LATE:
                 nc.vector.tensor_scalar(
-                    out=lin[:], in0=t[("u", r)][:], scalar1=c1[:, r : r + 1], scalar2=c0t[:, r : r + 1],
+                    out=lin[:], in0=u[:], scalar1=c1[:, r : r + 1], scalar2=c0t[:, r : r + 1],
                     op0=ALU.mult, op1=ALU.add,
                 )
             else:
                 nc.vector.tensor_scalar(
-                    out=lin[:], in0=t[("u", r)][:], scalar1=k1[:, r : r + 1], scalar2=nk0[:, r : r + 1],
+                    out=lin[:], in0=u[:], scalar1=k1[:, r : r + 1], scalar2=nk0[:, r : r + 1],
                     op0=ALU.mult, op1=ALU.add,
                 )
                 nc.vector.scalar_tensor_tensor(
-                    out=lin[:], in0=t[("u", r)][:], scalar=itau[:, r : r + 1], in1=lin[:],
+                    out=lin[:], in0=u[:], scalar=itau[:, r : r + 1], in1=lin[:],
                     op0=ALU.add, op1=ALU.mult,
                 )
-            t[("lin", r)] = lin
-            if r >= LATE_G:
-                a = t[("a", r)]
+            live[("lin", r)] = lin
+            if r >= LATE:
+                a = live[("a", r)]
                 nc.vector.tensor_scalar(
-                    out=a[:], in0=a[:], scalar1=cst[:, 48 + r : 49 + r], scalar2=None, op0=ALU.subtract
+                    out=a[:], in0=a[:], scalar1=cst[:, 48 + r : 49 + r], scalar2=None,
+                    op0=ALU.subtract,
                 )
 
-        def hn(r):
+        def h_of(r):
             return cn[1 + r // 4][:, :, P * (r % 4) : P * (r % 4 + 1)]
 
-        def pe_back(r):
+        def tensor_back(r):
             dt = psum.tile([P, BT, P], F32, name="dt%d" % r, tag="DT")
             rt = psum.tile([P, BT, P], F32, name="rt%d" % r, tag="RT")
             for i in range(BT):
+                cols = slice(P * i, P * (i + 1))
                 nc.tensor.matmul(
-                    out=rt[:, i, :], lhsT=t[("lin", r)][:, P * i : P * (i + 1)], rhs=ident_f[:],
-                    is_transpose=True, start=True, stop=(r >= LATE_R),
+                    out=rt[:, i, :], lhsT=live[("lin", r)][:, cols], rhs=ident_f[:],
+                    is_transpose=True, start=True, stop=(r >= LATE),
                 )
-                if r < LATE_R:
+                if r < LATE:
                     nc.tensor.matmul(
-                        out=rt[:, i, :], lhsT=t[("sq", r)][:, P * i : P * (i + 1)], rhs=ident_f[:],
+                        out=rt[:, i, :], lhsT=live[("sq", r)][:, cols], rhs=ident_f[:],
                         is_transpose=True, start=False, stop=True,
                     )
-            nc.tensor.matmul(out=dt[:], lhsT=ident_b[:], rhs=hn(r), start=True, stop=False)
-            if r < LATE_G:
+            nc.tensor.matmul(out=dt[:], lhsT=ident_b[:], rhs=h_of(r), start=True, stop=False)
+            if r < LATE:
                 nc.tensor.matmul(
                     out=dt[:], lhsT=neg0[:],
                     rhs=brow[:, P * r : P * (r + 1)].unsqueeze(1).to_broadcast([P, BT, P]),
@@ -271,89 +296,76 @@ def tile_ltccell_kernel(
                 )
             for i in range(BT):
                 nc.tensor.matmul(
-                    out=dt[:, i, :], lhsT=t[("a", r)][:, P * i : P * (i + 1)], rhs=ident_f[:],
+                    out=dt[:, i, :], lhsT=live[("a", r)][:, P * i : P * (i + 1)], rhs=ident_f[:],
                     is_transpose=True, start=False, stop=(i == BT - 1),
                 )
-            t[("rt", r)] = rt
-            t[("dt", r)] = dt
+            live[("rt", r)] = rt
+            live[("dt", r)] = dt
 
-        def s_exp(r):
+        def scalar_decay(r):
             dec = epi.tile([P, BT, P], F32, name="dec%d" % r, tag="dec")
             for i in range(BT):
                 nc.scalar.activation(
-                    out=dec[:, i, :], in_=t[("rt", r)][:, i, :], func=ACT.Exp, scale=cst[:, 64 + i : 65 + i]
+                    out=dec[:, i, :], in_=live[("rt", r)][:, i, :], func=ACT.Exp,
+                    scale=cst[:, 64 + i : 65 + i],
                 )
-            t[("dec", r)] = dec
+            live[("dec", r)] = dec
 
         out_v = out.rearrange("(i p) c -> p i c", p=P)
 
-        def v_blend(r):
-            if r % 2 == 0:
-                t["osb"] = epi.tile([P, BT, 2 * P], F32, name="osb%d" % r, tag="osb", bufs=3)
-            dec = t[("dec", r)]
-            nc.vector.scalar_tensor_tensor(
-                out=dec[:], in0=dec[:], scalar=-1.0, in1=t[("dt", r)][:], op0=ALU.add, op1=ALU.mult
-            )
+        def vector_blend(r):
             q = r % 2
+            if q == 0:
+                live["osb"] = epi.tile([P, BT, 2 * P], F32, name="osb%d" % r, tag="osb", bufs=3)
+            dec = live[("dec", r)]
+            nc.vector.scalar_tensor_tensor(
+                out=dec[:], in0=dec[:], scalar=-1.0, in1=live[("dt", r)][:],
+                op0=ALU.add, op1=ALU.mult,
+            )
             nc.vector.tensor_tensor(
-                out=t["osb"][:, :, P * q : P * (q + 1)], in0=dec[:], in1=hn(r), op=ALU.add
+                out=live["osb"][:, :, P * q : P * (q + 1)], in0=dec[:], in1=h_of(r), op=ALU.add
             )
             if q == 1:
-                nc.sync.dma_start(out=out_v[:, :, P * (r - 1) : P * (r + 1)], in_=t["osb"][:])
-
-        def by_scalar(sp, g):
-            return (sp, g) in S_UNITS
-
-        def s_prep(units):
-            for sp, g in units:
-                new_grp(sp, g)
-                if by_scalar(sp, g):
-                    copy(sp, g, 1, "S")
-
-        def v_prep(units):
-            for sp, g in units:
-                copy(sp, g, 0, "V")
-                if not by_scalar(sp, g):
-                    copy(sp, g, 1, "V")
-            for sp, g in units:
-                quantise(sp, g)
+                nc.sync.dma_start(out=out_v[:, :, P * (r - 1) : P * (r + 1)], in_=live["osb"][:])
 
         for g in range(PASSES):
-            s_prep([(0, g)])
-            v_prep([(0, g)])
+            scalar_prep([(0, g)])
+            vector_prep([(0, g)])
             for r in range(2):
                 for m in range(2):
                     mx_pass(r, m, g)
+
         stream = [(sp, g) for sp in range(1, len(SPANS)) for g in range(PASSES)]
-        sets = [[] for j in range(ROUNDS - 2)]
-        pos = 0
+        periods = ROUNDS - 2
+        sets = [[] for j in range(periods)]
         total = sum(SPANS[sp][1] for sp, g in stream)
+        pos = 0
         done = 0
-        for j in range(ROUNDS - 2):
-            target = total * (j + 1) / (ROUNDS - 2)
+        for j in range(periods):
+            target = total * (j + 1) / periods
             while pos < len(stream) and (done < target or SPANS[stream[pos][0]][0] <= j + 2):
                 sets[j].append(stream[pos])
                 done += SPANS[stream[pos][0]][1]
                 pos += 1
         assert pos == len(stream)
-        s_prep(sets[0])
 
+        scalar_prep(sets[0])
         for j in range(ROUNDS + 1):
             if j >= 1:
-                pe_back(j - 1)
+                tensor_back(j - 1)
             if 2 <= j + 1 < ROUNDS:
                 for m in (1, 0):
                     for g in range(PASSES):
                         mx_pass(j + 1, m, g)
             if j < ROUNDS:
-                s_front(j)
+                scalar_front(j)
             if j >= 1:
-                s_exp(j - 1)
-            if j + 1 < len(sets):
-                s_prep(sets[j + 1])
-            if j < len(sets):
-                v_prep(sets[j])
+                scalar_decay(j - 1)
+            if j + 1 < periods:
+                scalar_prep(sets[j + 1])
+            if j < periods:
+                vector_prep(sets[j])
             if j < ROUNDS:
-                v_lin(j)
+                vector_front(j)
             if j >= 1:
-                v_blend(j - 1)
+                vector_blend(j - 1)

@@ -1,4 +1,3 @@
-import math
 from contextlib import ExitStack
 
 import concourse.mybir as mybir
@@ -24,15 +23,26 @@ EPS = 1e-6
 FLOPS = 2 * 2 * B * K * H
 
 SLAB = 512
-RAW_BUFS = 18
-SPANS = tuple((r, 2) for r in range(0, ROUNDS - 2, 2)) + ((ROUNDS - 2, 1), (ROUNDS - 1, 1))
-GRP_BUFS = {2: 4, 1: 4}
-WQ_BUFS = {2: 3, 1: 2}
-LATE = 10
+QS = SLAB // P
+RAW_BUFS = 16
+GROUPS = 2 * H // SLAB
+STEPS = GROUPS * QS
+WHOLE = ((0, SLAB),)
+LAST = ((0, 2 * P), (2 * P, P), (3 * P, P))
+GRP_BUFS = {SLAB: 5, 2 * P: 3, P: 4}
+WQ_BUFS = {SLAB: 3, 2 * P: 1, P: 2}
 
 
-def by_scalar(sp, g):
-    return g < PASSES - 1 and (g > 0 or sp % 2 == 1)
+def parts_of(w):
+    return LAST if w == GROUPS - 1 else WHOLE
+
+
+def scalar_columns(w, g, n):
+    if w == 0:
+        return 3 * n // 4
+    if w % 2 == 0:
+        return n if g % 2 == 1 else n // 2
+    return n // 2 if g % 2 == 1 else 0
 
 
 def tile_ltccell_kernel(
@@ -73,75 +83,48 @@ def tile_ltccell_kernel(
         make_identity(nc, ident_b[:])
 
         cn = []
-        for g in range(PASSES):
+
+        def load_c(g):
             src = x if g == 0 else h[:, K_PASS * (g - 1) : K_PASS * g]
             cng = const.tile([P, BT, K_PASS], BF16, name="cn%d" % g)
             nc.sync.dma_start(out=cng[:], in_=src.rearrange("(i p) k -> p i k", p=P))
             cn.append(cng)
-        chunks = [
-            (c0, g, m) for c0 in range(0, H, SLAB) for g in range(PASSES) for m in range(2)
-        ]
+
+        chunks = [(w, g) for w in range(GROUPS) for g in range(PASSES)]
         raws = {}
         ring = {"next": 0, "free": RAW_BUFS}
 
         def load_more():
             while ring["next"] < len(chunks) and ring["free"] > 0:
-                c0, g, m = chunks[ring["next"]]
+                w, g = chunks[ring["next"]]
                 raw = rawp.tile(
                     [P, PACK, SLAB], BF16, name="raw%d" % ring["next"], tag="raw", bufs=RAW_BUFS
                 )
+                c0 = SLAB * (w // 2)
                 nc.sync.dma_start(
                     out=raw[:],
-                    in_=weights[m][K_PASS * g : K_PASS * (g + 1), c0 : c0 + SLAB].rearrange(
+                    in_=weights[w % 2][K_PASS * g : K_PASS * (g + 1), c0 : c0 + SLAB].rearrange(
                         "(p j) w -> p j w", j=PACK
                     ),
                 )
-                for r in range(c0 // P, (c0 + SLAB) // P):
-                    raws[(r, g, m)] = (raw, c0)
+                raws[(w, g)] = raw
+                if w == 0:
+                    load_c(g)
                 ring["free"] -= 1
                 ring["next"] += 1
 
         load_more()
 
-        pst = psum.tile([P, P], BF16, name="pst", tag="DT")
-        nc.tensor.transpose(pst[:], vecs[:], ident_b[:])
-        cst = const.tile([P, P], F32, name="cst")
-        nc.vector.tensor_copy(out=cst[:], in_=pst[:])
-        itau = const.tile([P, 16], F32, name="itau")
-        nc.scalar.activation(out=itau[:], in_=cst[:, 32:48], func=ACT.Exp, scale=-1.0)
-        t1n = const.tile([P, 16], F32, name="t1n")
-        nc.vector.tensor_scalar(
-            out=t1n[:], in0=itau[:], scalar1=-EPS, scalar2=-1.0, op0=ALU.mult, op1=ALU.add
-        )
-        nk0 = const.tile([P, 16], F32, name="nk0")
-        nc.vector.reciprocal(out=nk0[:], in_=t1n[:])
-        sqe = const.tile([P, 16], F32, name="sqe")
-        nc.vector.tensor_scalar(
-            out=sqe[:], in0=nk0[:], scalar1=-math.sqrt(EPS), scalar2=None, op0=ALU.mult
-        )
-        c1 = const.tile([P, 16], F32, name="c1")
-        nc.vector.scalar_tensor_tensor(
-            out=c1[:], in0=nk0[:], scalar=-1.0, in1=nk0[:], op0=ALU.mult, op1=ALU.mult
-        )
-        nbt = const.tile([P, 16], F32, name="nbt")
-        nc.vector.tensor_scalar(
-            out=nbt[:], in0=cst[:, 16:32], scalar1=-1.0, scalar2=None, op0=ALU.mult
-        )
-        k1 = const.tile([P, 16], F32, name="k1")
-        nc.vector.tensor_tensor(out=k1[:], in0=sqe[:], in1=sqe[:], op=ALU.mult)
-        c0t = const.tile([P, 16], F32, name="c0t")
-        nc.vector.tensor_tensor(out=c0t[:], in0=nk0[:], in1=itau[:], op=ALU.mult)
-
         cq = []
         cs = []
-        bank_tags = ("F", "A", "RT", "DT")
-        for g in range(PASSES):
+
+        def c_pass(g):
             cg = cgp.tile([P, B * PACK], BF16, name="cg%d" % g, tag="cg", align_bytes=64)
             cgf = cg[:].bitcast(F32).rearrange("p (b u) -> p b u", u=2)
             cnf = cn[g][:].bitcast(F32).rearrange("p i (q u) -> p i u q", u=2)
             for half in range(2):
                 xt = psum.tile(
-                    [P, 2, 2, P], F32, name="xt%d_%d" % (g, half), tag=bank_tags[(2 * g + half) % 4]
+                    [P, 2, 2, P], F32, name="xt%d_%d" % (g, half), tag=("RT", "DT")[half]
                 )
                 for il in range(2):
                     for u in range(2):
@@ -164,208 +147,235 @@ def tile_ltccell_kernel(
         wqs = {}
         live = {}
 
-        def new_grp(sp, g):
-            nr = SPANS[sp][1]
-            grps[(sp, g)] = grpp.tile(
-                [P, 2, nr * P, PACK], BF16, name="grp%d_%d" % (sp, g), tag="grp%d" % nr,
-                align_bytes=64, bufs=GRP_BUFS[nr],
-            )
-
-        def regroup(sp, g, m, engine_copy):
-            r0, nr = SPANS[sp]
-            raw, c0 = raws[(r0, g, m)]
-            o = P * r0 - c0
+        def regroup(unit, lo, n, engine_copy):
+            w, pt, g = unit
+            c0 = parts_of(w)[pt][0]
             engine_copy(
-                out=grps[(sp, g)][:, m, :, :].rearrange("p (c i) t -> p c t i", i=4),
-                in_=raw[:, :, o : o + nr * P].rearrange("p t (c i) -> p c t i", i=4),
+                out=grps[unit][:, lo : lo + n, :].rearrange("p (c i) t -> p c t i", i=4),
+                in_=raws[(w, g)][:, :, c0 + lo : c0 + lo + n].rearrange("p t (c i) -> p c t i", i=4),
             )
-            if o + nr * P == SLAB:
-                ring["free"] += 1
-                load_more()
-
-        def quantise(sp, g):
-            r0, nr = SPANS[sp]
-            wq = wqp.tile(
-                [P, 2 * nr * P], U32, name="wq%d_%d" % (sp, g), tag="wq%d_%d" % (nr, g),
-                align_bytes=64, bufs=WQ_BUFS[nr],
-            )
-            ws = wqp.tile(
-                [P, 2 * nr * P], U8, name="ws%d_%d" % (sp, g), tag="ws%d_%d" % (nr, g),
-                align_bytes=64, bufs=WQ_BUFS[nr],
-            )
-            nc.vector.quantize_mx(
-                out=wq[:].bitcast(FP8X4), scales=ws[:],
-                in_=grps[(sp, g)][:].rearrange("p m w t -> p (m w t)"),
-            )
-            for r in range(r0, r0 + nr):
-                for m in range(2):
-                    wqs[(r, g, m)] = (wq, ws, (m * nr + r - r0) * P)
 
         def scalar_prep(units):
-            for sp, g in units:
-                new_grp(sp, g)
-                if by_scalar(sp, g):
-                    regroup(sp, g, 1, nc.scalar.copy)
-
-        def vector_prep(units):
-            for sp, g in units:
-                regroup(sp, g, 0, nc.vector.tensor_copy)
-                if not by_scalar(sp, g):
-                    regroup(sp, g, 1, nc.vector.tensor_copy)
-            for sp, g in units:
-                quantise(sp, g)
-
-        def mx_pass(r, m, g):
-            if g == 0:
-                live[("z", r, m)] = psum.tile(
-                    [P, B], F32, name="ps%d_%d" % (m, r), tag=("F", "A")[m]
+            for unit in units:
+                w, pt, g = unit
+                n = parts_of(w)[pt][1]
+                grps[unit] = grpp.tile(
+                    [P, n, PACK], BF16, name="grp%d_%d_%d" % unit, tag="grp%d" % n,
+                    align_bytes=64, bufs=GRP_BUFS[n],
                 )
-            wq, ws, o = wqs[(r, g, m)]
+                ns = scalar_columns(w, g, n)
+                for lo in range(0, ns, 2 * P):
+                    regroup(unit, lo, min(2 * P, ns - lo), nc.scalar.copy)
+
+        def vector_copy(units):
+            for unit in units:
+                w, pt, g = unit
+                n = parts_of(w)[pt][1]
+                ns = scalar_columns(w, g, n)
+                if ns < n:
+                    regroup(unit, ns, n - ns, nc.vector.tensor_copy)
+                if pt == len(parts_of(w)) - 1:
+                    ring["free"] += 1
+                    load_more()
+
+        def quantise(units):
+            for unit in units:
+                w, pt, g = unit
+                c0, n = parts_of(w)[pt]
+                wq = wqp.tile(
+                    [P, n], U32, name="wq%d_%d_%d" % unit, tag="wq%d_%d" % (n, g),
+                    align_bytes=64, bufs=WQ_BUFS[n],
+                )
+                ws = wqp.tile(
+                    [P, n], U8, name="ws%d_%d_%d" % unit, tag="ws%d_%d" % (n, g),
+                    align_bytes=64, bufs=WQ_BUFS[n],
+                )
+                nc.vector.quantize_mx(
+                    out=wq[:].bitcast(FP8X4), scales=ws[:],
+                    in_=grps[unit][:].rearrange("p w t -> p (w t)"),
+                )
+                for q in range(c0 // P, (c0 + n) // P):
+                    wqs[(w, q, g)] = (wq, ws, P * q - c0)
+
+        def mx_pass(t, g):
+            w, q = divmod(t, QS)
+            if g == 0:
+                live[("z", t)] = psum.tile([P, B], F32, name="z%d" % t, tag="Z", bufs=4)
+            wq, ws, o = wqs[(w, q, g)]
             nc.tensor.matmul_mx(
-                out=live[("z", r, m)][:],
+                out=live[("z", t)][:],
                 lhsT=wq[:, o : o + P].bitcast(FP8X4), lhsT_scale=ws[:, o : o + P],
                 rhs=cq[g][:].bitcast(FP8X4), rhs_scale=cs[g][:],
                 start=(g == 0), stop=(g == PASSES - 1),
             )
 
-        def scalar_front(r):
-            a = epi.tile([P, B], F32, name="a%d" % r, tag="a")
-            nc.scalar.activation(
-                out=a[:], in_=live[("z", r, 1)][:], func=ACT.Tanh, bias=nbt[:, r : r + 1], scale=-1.0
-            )
-            u = epi.tile([P, B], F32, name="u%d" % r, tag="u")
-            nc.scalar.activation(
-                out=u[:], in_=live[("z", r, 0)][:], func=ACT.Abs, bias=cst[:, r : r + 1]
-            )
-            nc.scalar.activation(out=u[:], in_=u[:], func=ACT.Tanh)
-            live[("a", r)] = a
-            live[("u", r)] = u
-            if r < LATE:
-                sq = epi.tile([P, B], F32, name="sq%d" % r, tag="sq")
-                nc.scalar.activation(out=sq[:], in_=u[:], func=ACT.Square, scale=sqe[:, r : r + 1])
-                live[("sq", r)] = sq
+        def round_of(t):
+            w, q = divmod(t, QS)
+            return w % 2, QS * (w // 2) + q
 
-        def vector_front(r):
-            lin = epi.tile([P, B], F32, name="lin%d" % r, tag="lin")
-            u = live[("u", r)]
-            if r < LATE:
-                nc.vector.tensor_scalar(
-                    out=lin[:], in0=u[:], scalar1=c1[:, r : r + 1], scalar2=c0t[:, r : r + 1],
-                    op0=ALU.mult, op1=ALU.add,
-                )
+        def h_of(r, n):
+            return cn[1 + r // 4][:, :, P * (r % 4) : P * (r % 4 + n)]
+
+        def scalar_front(t):
+            m, r = round_of(t)
+            z = live[("z", t)]
+            if m == 0:
+                u = epi.tile([P, B], F32, name="u%d" % r, tag="u")
+                nc.scalar.activation(out=u[:], in_=z[:], func=ACT.Abs, bias=cst[:, r : r + 1])
+                nc.scalar.activation(out=u[:], in_=u[:], func=ACT.Tanh, bias=epsc[:])
+                live[("u", r)] = u
             else:
-                nc.vector.tensor_scalar(
-                    out=lin[:], in0=u[:], scalar1=k1[:, r : r + 1], scalar2=nk0[:, r : r + 1],
-                    op0=ALU.mult, op1=ALU.add,
+                a = epi.tile([P, B], F32, name="a%d" % r, tag="a")
+                nc.scalar.activation(
+                    out=a[:], in_=z[:], func=ACT.Tanh, bias=nbt[:, r : r + 1], scale=-1.0
                 )
-                nc.vector.scalar_tensor_tensor(
-                    out=lin[:], in0=u[:], scalar=itau[:, r : r + 1], in1=lin[:],
-                    op0=ALU.add, op1=ALU.mult,
-                )
-            live[("lin", r)] = lin
-            if r >= LATE:
-                a = live[("a", r)]
-                nc.vector.tensor_scalar(
-                    out=a[:], in0=a[:], scalar1=cst[:, 48 + r : 49 + r], scalar2=None,
-                    op0=ALU.subtract,
-                )
+                live[("a", r)] = a
 
-        def h_of(r):
-            return cn[1 + r // 4][:, :, P * (r % 4) : P * (r % 4 + 1)]
-
-        def tensor_back(r):
-            dt = psum.tile([P, BT, P], F32, name="dt%d" % r, tag="DT")
-            rt = psum.tile([P, BT, P], F32, name="rt%d" % r, tag="RT")
-            for i in range(BT):
-                cols = slice(P * i, P * (i + 1))
-                nc.tensor.matmul(
-                    out=rt[:, i, :], lhsT=live[("lin", r)][:, cols], rhs=ident_f[:],
-                    is_transpose=True, start=True, stop=(r >= LATE),
+        def vector_front(t):
+            m, r = round_of(t)
+            if m == 0:
+                lin = epi.tile([P, B], F32, name="lin%d" % r, tag="lin")
+                nc.vector.tensor_scalar(
+                    out=lin[:], in0=live[("u", r)][:], scalar1=c1[:, r : r + 1],
+                    scalar2=c0t[:, r : r + 1], op0=ALU.mult, op1=ALU.add,
                 )
-                if r < LATE:
-                    nc.tensor.matmul(
-                        out=rt[:, i, :], lhsT=live[("sq", r)][:, cols], rhs=ident_f[:],
-                        is_transpose=True, start=False, stop=True,
+                live[("lin", r)] = lin
+
+        def tensor_back(t):
+            m, r = round_of(t)
+            if m == 0:
+                rt = psum.tile([P, BT, P], F32, name="rt%d" % r, tag="RT")
+                for i in range(BT):
+                    nc.tensor.transpose(
+                        rt[:, i, :], live[("lin", r)][:, P * i : P * (i + 1)], ident_f[:]
                     )
-            nc.tensor.matmul(out=dt[:], lhsT=ident_b[:], rhs=h_of(r), start=True, stop=False)
-            if r < LATE:
+                live[("rt", r)] = rt
+            else:
+                dt = psum.tile([P, BT, P], F32, name="dt%d" % r, tag="DT")
+                nc.tensor.matmul(
+                    out=dt[:], lhsT=ident_b[:], rhs=h_of(r, 1), start=True, stop=False
+                )
                 nc.tensor.matmul(
                     out=dt[:], lhsT=neg0[:],
                     rhs=brow[:, P * r : P * (r + 1)].unsqueeze(1).to_broadcast([P, BT, P]),
                     start=False, stop=False,
                 )
-            for i in range(BT):
-                nc.tensor.matmul(
-                    out=dt[:, i, :], lhsT=live[("a", r)][:, P * i : P * (i + 1)], rhs=ident_f[:],
-                    is_transpose=True, start=False, stop=(i == BT - 1),
-                )
-            live[("rt", r)] = rt
-            live[("dt", r)] = dt
+                for i in range(BT):
+                    nc.tensor.matmul(
+                        out=dt[:, i, :], lhsT=live[("a", r)][:, P * i : P * (i + 1)],
+                        rhs=ident_f[:], is_transpose=True, start=False, stop=(i == BT - 1),
+                    )
+                live[("dt", r)] = dt
 
-        def scalar_decay(r):
-            dec = epi.tile([P, BT, P], F32, name="dec%d" % r, tag="dec")
-            for i in range(BT):
-                nc.scalar.activation(
-                    out=dec[:, i, :], in_=live[("rt", r)][:, i, :], func=ACT.Exp,
-                    scale=cst[:, 64 + i : 65 + i],
-                )
-            live[("dec", r)] = dec
+        def scalar_decay(t):
+            m, r = round_of(t)
+            if m == 0:
+                dec = epi.tile([P, BT, P], F32, name="dec%d" % r, tag="dec", bufs=6)
+                for i in range(BT):
+                    nc.scalar.activation(
+                        out=dec[:, i, :], in_=live[("rt", r)][:, i, :], func=ACT.Exp,
+                        scale=cst[:, 64 + i : 65 + i],
+                    )
+                live[("dec", r)] = dec
 
         out_v = out.rearrange("(i p) c -> p i c", p=P)
 
-        def vector_blend(r):
-            q = r % 2
-            if q == 0:
+        def vector_blend(t):
+            m, r = round_of(t)
+            if m == 0:
+                return
+            if r % 2 == 0:
                 live["osb"] = epi.tile([P, BT, 2 * P], F32, name="osb%d" % r, tag="osb", bufs=3)
-            dec = live[("dec", r)]
+            osb = live["osb"]
+            mine = osb[:, :, P * (r % 2) : P * (r % 2 + 1)]
             nc.vector.scalar_tensor_tensor(
-                out=dec[:], in0=dec[:], scalar=-1.0, in1=live[("dt", r)][:],
+                out=mine, in0=live[("dec", r)][:], scalar=-1.0, in1=live[("dt", r)][:],
                 op0=ALU.add, op1=ALU.mult,
             )
-            nc.vector.tensor_tensor(
-                out=live["osb"][:, :, P * q : P * (q + 1)], in0=dec[:], in1=h_of(r), op=ALU.add
-            )
-            if q == 1:
-                nc.sync.dma_start(out=out_v[:, :, P * (r - 1) : P * (r + 1)], in_=live["osb"][:])
+            if r >= ROUNDS - 2:
+                nc.vector.tensor_tensor(out=mine, in0=mine, in1=h_of(r, 1), op=ALU.add)
+            elif r % 2 == 1:
+                nc.vector.tensor_tensor(out=osb[:], in0=osb[:], in1=h_of(r - 1, 2), op=ALU.add)
+            if r % 2 == 1:
+                nc.sync.dma_start(out=out_v[:, :, P * (r - 1) : P * (r + 1)], in_=osb[:])
 
         for g in range(PASSES):
-            scalar_prep([(0, g)])
-            vector_prep([(0, g)])
-            for r in range(2):
-                for m in range(2):
-                    mx_pass(r, m, g)
+            unit = [(0, 0, g)]
+            scalar_prep(unit)
+            vector_copy(unit)
+            c_pass(g)
+            quantise(unit)
+            for q in range(QS):
+                mx_pass(q, g)
 
-        stream = [(sp, g) for sp in range(1, len(SPANS)) for g in range(PASSES)]
-        periods = ROUNDS - 2
-        sets = [[] for j in range(periods)]
-        total = sum(SPANS[sp][1] for sp, g in stream)
+        pst = psum.tile([P, P], BF16, name="pst", tag="DT")
+        nc.tensor.transpose(pst[:], vecs[:], ident_b[:])
+        cst = const.tile([P, P], F32, name="cst")
+        nc.vector.tensor_copy(out=cst[:], in_=pst[:])
+        itau = const.tile([P, 16], F32, name="itau")
+        nc.scalar.activation(out=itau[:], in_=cst[:, 32:48], func=ACT.Exp, scale=-1.0)
+        t1n = const.tile([P, 16], F32, name="t1n")
+        nc.vector.tensor_scalar(
+            out=t1n[:], in0=itau[:], scalar1=-EPS, scalar2=-1.0, op0=ALU.mult, op1=ALU.add
+        )
+        nk0 = const.tile([P, 16], F32, name="nk0")
+        nc.vector.reciprocal(out=nk0[:], in_=t1n[:])
+        c1 = const.tile([P, 16], F32, name="c1")
+        nc.vector.scalar_tensor_tensor(
+            out=c1[:], in0=nk0[:], scalar=-1.0, in1=nk0[:], op0=ALU.mult, op1=ALU.mult
+        )
+        nbt = const.tile([P, 16], F32, name="nbt")
+        nc.vector.tensor_scalar(
+            out=nbt[:], in0=cst[:, 16:32], scalar1=-1.0, scalar2=None, op0=ALU.mult
+        )
+        c0t = const.tile([P, 16], F32, name="c0t")
+        nc.vector.scalar_tensor_tensor(
+            out=c0t[:], in0=nk0[:], scalar=EPS, in1=itau[:], op0=ALU.mult, op1=ALU.add
+        )
+        nc.vector.tensor_tensor(out=c0t[:], in0=c0t[:], in1=nk0[:], op=ALU.mult)
+        epsc = const.tile([P, 1], F32, name="epsc")
+        nc.vector.tensor_scalar(
+            out=epsc[:], in0=itau[:, 0:1], scalar1=0.0, scalar2=EPS, op0=ALU.mult, op1=ALU.add
+        )
+
+        stream = [
+            (w, pt, g)
+            for w in range(1, GROUPS)
+            for pt in range(len(parts_of(w)))
+            for g in range(PASSES)
+        ]
+        sets = [[] for t in range(STEPS + 1)]
+        total = (GROUPS - 1) * PASSES * SLAB
         pos = 0
         done = 0
-        for j in range(periods):
-            target = total * (j + 1) / periods
-            while pos < len(stream) and (done < target or SPANS[stream[pos][0]][0] <= j + 2):
-                sets[j].append(stream[pos])
-                done += SPANS[stream[pos][0]][1]
+        for t in range(STEPS - 2):
+            target = total * (t + 2) / (STEPS - 1)
+            while pos < len(stream):
+                w, pt, g = stream[pos]
+                c0, n = parts_of(w)[pt]
+                if done >= target and QS * w + c0 // P - 2 > t:
+                    break
+                sets[t].append(stream[pos])
+                done += n
                 pos += 1
         assert pos == len(stream)
 
         scalar_prep(sets[0])
-        for j in range(ROUNDS + 1):
-            if j >= 1:
-                tensor_back(j - 1)
-            if 2 <= j + 1 < ROUNDS:
-                for m in (1, 0):
-                    for g in range(PASSES):
-                        mx_pass(j + 1, m, g)
-            if j < ROUNDS:
-                scalar_front(j)
-            if j >= 1:
-                scalar_decay(j - 1)
-            if j + 1 < periods:
-                scalar_prep(sets[j + 1])
-            if j < periods:
-                vector_prep(sets[j])
-            if j < ROUNDS:
-                vector_front(j)
-            if j >= 1:
-                vector_blend(j - 1)
+        for t in range(STEPS + 1):
+            if t >= 1:
+                tensor_back(t - 1)
+            if QS <= t + 1 < STEPS:
+                for g in range(PASSES):
+                    mx_pass(t + 1, g)
+            if t < STEPS:
+                scalar_front(t)
+            if t >= 1:
+                scalar_decay(t - 1)
+            if t < STEPS:
+                scalar_prep(sets[t + 1])
+            vector_copy(sets[t])
+            quantise(sets[t])
+            if t < STEPS:
+                vector_front(t)
+            if t >= 1:
+                vector_blend(t - 1)

@@ -23,26 +23,32 @@ EPS = 1e-6
 FLOPS = 2 * 2 * B * K * H
 
 SLAB = 512
-QS = SLAB // P
 RAW_BUFS = 16
-GROUPS = 2 * H // SLAB
-STEPS = GROUPS * QS
-WHOLE = ((0, SLAB),)
-LAST = ((0, 2 * P), (2 * P, P), (3 * P, P))
-GRP_BUFS = {SLAB: 5, 2 * P: 3, P: 4}
-WQ_BUFS = {SLAB: 3, 2 * P: 1, P: 2}
+FIRST = SLAB // P
+
+def group_list():
+    groups = [((0, 0, SLAB),), ((1, 0, SLAB),)]
+    groups += [((0, P * r, 2 * P), (1, P * r, 2 * P)) for r in range(FIRST, ROUNDS - 2, 2)]
+    groups += [((0, P * r, P), (1, P * r, P)) for r in range(ROUNDS - 2, ROUNDS)]
+    return groups
 
 
-def parts_of(w):
-    return LAST if w == GROUPS - 1 else WHOLE
+GROUPS = group_list()
+GRP_BUFS = {SLAB: 6, 2 * P: 6}
+WQ_BUFS = {SLAB: 3, 2 * P: 2}
 
 
-def scalar_columns(w, g, n):
+def columns_of(w):
+    return sum(n for m, c0, n in GROUPS[w])
+
+
+def scalar_columns(w, g):
+    n = columns_of(w)
     if w == 0:
         return 3 * n // 4
-    if w % 2 == 0:
-        return n if g % 2 == 1 else n // 2
-    return n // 2 if g % 2 == 1 else 0
+    if w == 1:
+        return n // 2 if g >= 2 else 0
+    return n // 2 if g < 4 else 0
 
 
 def tile_ltccell_kernel(
@@ -90,25 +96,25 @@ def tile_ltccell_kernel(
             nc.sync.dma_start(out=cng[:], in_=src.rearrange("(i p) k -> p i k", p=P))
             cn.append(cng)
 
-        chunks = [(w, g) for w in range(GROUPS) for g in range(PASSES)]
+        chunks = [(0, g, m) for m in range(2) for g in range(PASSES)]
+        chunks += [(c0, g, m) for c0 in range(SLAB, H, SLAB) for g in range(PASSES) for m in range(2)]
         raws = {}
         ring = {"next": 0, "free": RAW_BUFS}
 
         def load_more():
             while ring["next"] < len(chunks) and ring["free"] > 0:
-                w, g = chunks[ring["next"]]
+                c0, g, m = chunks[ring["next"]]
                 raw = rawp.tile(
                     [P, PACK, SLAB], BF16, name="raw%d" % ring["next"], tag="raw", bufs=RAW_BUFS
                 )
-                c0 = SLAB * (w // 2)
                 nc.sync.dma_start(
                     out=raw[:],
-                    in_=weights[w % 2][K_PASS * g : K_PASS * (g + 1), c0 : c0 + SLAB].rearrange(
+                    in_=weights[m][K_PASS * g : K_PASS * (g + 1), c0 : c0 + SLAB].rearrange(
                         "(p j) w -> p j w", j=PACK
                     ),
                 )
-                raws[(w, g)] = raw
-                if w == 0:
+                raws[(c0 // SLAB, g, m)] = raw
+                if ring["next"] < PASSES:
                     load_c(g)
                 ring["free"] -= 1
                 ring["next"] += 1
@@ -117,10 +123,10 @@ def tile_ltccell_kernel(
 
         cq = []
         cs = []
+        xts = {}
+        cgs = {}
 
-        def c_pass(g):
-            cg = cgp.tile([P, B * PACK], BF16, name="cg%d" % g, tag="cg", align_bytes=64)
-            cgf = cg[:].bitcast(F32).rearrange("p (b u) -> p b u", u=2)
+        def c_transpose(g):
             cnf = cn[g][:].bitcast(F32).rearrange("p i (q u) -> p i u q", u=2)
             for half in range(2):
                 xt = psum.tile(
@@ -131,15 +137,24 @@ def tile_ltccell_kernel(
                         nc.tensor.transpose(
                             xt[:, u, il, :], cnf[:, 2 * half + il, u, :], ident_f[:]
                         )
+                xts[(g, half)] = xt
+
+        def c_copies(g):
+            cg = cgp.tile([P, B * PACK], BF16, name="cg%d" % g, tag="cg", align_bytes=64)
+            cgf = cg[:].bitcast(F32).rearrange("p (b u) -> p b u", u=2)
+            for half in range(2):
                 dst = cgf[:, 256 * half : 256 * half + 256, :]
-                src = xt[:].rearrange("p u i b -> p (i b) u")
+                src = xts[(g, half)][:].rearrange("p u i b -> p (i b) u")
                 if half == 0:
                     nc.vector.tensor_copy(out=dst, in_=src)
                 else:
                     nc.scalar.copy(out=dst, in_=src)
+            cgs[g] = cg
+
+        def c_quantise(g):
             cqg = const.tile([P, B], U32, name="cq%d" % g, align_bytes=64)
             csg = const.tile([P, B], U8, name="cs%d" % g, align_bytes=64)
-            nc.vector.quantize_mx(out=cqg[:].bitcast(FP8X4), scales=csg[:], in_=cg[:])
+            nc.vector.quantize_mx(out=cqg[:].bitcast(FP8X4), scales=csg[:], in_=cgs[g][:])
             cq.append(cqg)
             cs.append(csg)
 
@@ -147,235 +162,271 @@ def tile_ltccell_kernel(
         wqs = {}
         live = {}
 
-        def regroup(unit, lo, n, engine_copy):
-            w, pt, g = unit
-            c0 = parts_of(w)[pt][0]
-            engine_copy(
-                out=grps[unit][:, lo : lo + n, :].rearrange("p (c i) t -> p c t i", i=4),
-                in_=raws[(w, g)][:, :, c0 + lo : c0 + lo + n].rearrange("p t (c i) -> p c t i", i=4),
-            )
+        def regroup(w, g, lo, hi, engine_copy):
+            at = 0
+            for m, c0, n in GROUPS[w]:
+                a = max(lo, at)
+                b = min(hi, at + n)
+                if a < b:
+                    o = c0 % SLAB + a - at
+                    engine_copy(
+                        out=grps[(w, g)][:, a:b, :].rearrange("p (c i) t -> p c t i", i=4),
+                        in_=raws[(c0 // SLAB, g, m)][:, :, o : o + b - a].rearrange(
+                            "p t (c i) -> p c t i", i=4
+                        ),
+                    )
+                at += n
 
         def scalar_prep(units):
-            for unit in units:
-                w, pt, g = unit
-                n = parts_of(w)[pt][1]
-                grps[unit] = grpp.tile(
-                    [P, n, PACK], BF16, name="grp%d_%d_%d" % unit, tag="grp%d" % n,
-                    align_bytes=64, bufs=GRP_BUFS[n],
+            for w, g in units:
+                n = columns_of(w)
+                grps[(w, g)] = grpp.tile(
+                    [P, n, PACK], BF16, name="grp%d_%d" % (w, g), tag="grp%d" % n, align_bytes=64,
+                    bufs=GRP_BUFS[n],
                 )
-                ns = scalar_columns(w, g, n)
-                for lo in range(0, ns, 2 * P):
-                    regroup(unit, lo, min(2 * P, ns - lo), nc.scalar.copy)
+                for a in range(n - scalar_columns(w, g), n, 2 * P):
+                    regroup(w, g, a, min(n, a + 2 * P), nc.scalar.copy)
 
-        def vector_copy(units):
-            for unit in units:
-                w, pt, g = unit
-                n = parts_of(w)[pt][1]
-                ns = scalar_columns(w, g, n)
-                if ns < n:
-                    regroup(unit, ns, n - ns, nc.vector.tensor_copy)
-                if pt == len(parts_of(w)) - 1:
+        def vector_copies(w, g):
+            n = columns_of(w)
+            regroup(w, g, 0, n - scalar_columns(w, g), nc.vector.tensor_copy)
+            for m, c0, size in GROUPS[w]:
+                if (c0 + size) % SLAB == 0:
                     ring["free"] += 1
-                    load_more()
+            load_more()
 
-        def quantise(units):
-            for unit in units:
-                w, pt, g = unit
-                c0, n = parts_of(w)[pt]
-                wq = wqp.tile(
-                    [P, n], U32, name="wq%d_%d_%d" % unit, tag="wq%d_%d" % (n, g),
-                    align_bytes=64, bufs=WQ_BUFS[n],
-                )
-                ws = wqp.tile(
-                    [P, n], U8, name="ws%d_%d_%d" % unit, tag="ws%d_%d" % (n, g),
-                    align_bytes=64, bufs=WQ_BUFS[n],
-                )
-                nc.vector.quantize_mx(
-                    out=wq[:].bitcast(FP8X4), scales=ws[:],
-                    in_=grps[unit][:].rearrange("p w t -> p (w t)"),
-                )
-                for q in range(c0 // P, (c0 + n) // P):
-                    wqs[(w, q, g)] = (wq, ws, P * q - c0)
+        def quantise(w, g):
+            n = columns_of(w)
+            wq = wqp.tile(
+                [P, n], U32, name="wq%d_%d" % (w, g), tag="wq%d_%d" % (n, g), align_bytes=64,
+                bufs=WQ_BUFS[n],
+            )
+            ws = wqp.tile(
+                [P, n], U8, name="ws%d_%d" % (w, g), tag="ws%d_%d" % (n, g), align_bytes=64,
+                bufs=WQ_BUFS[n],
+            )
+            nc.vector.quantize_mx(
+                out=wq[:].bitcast(FP8X4), scales=ws[:],
+                in_=grps[(w, g)][:].rearrange("p w t -> p (w t)"),
+            )
+            at = 0
+            for m, c0, size in GROUPS[w]:
+                for i in range(size // P):
+                    wqs[(c0 // P + i, g, m)] = (wq, ws, at + P * i)
+                at += size
 
-        def mx_pass(t, g):
-            w, q = divmod(t, QS)
+        def mx_pass(r, m, g):
             if g == 0:
-                live[("z", t)] = psum.tile([P, B], F32, name="z%d" % t, tag="Z", bufs=4)
-            wq, ws, o = wqs[(w, q, g)]
+                live[("z", r, m)] = psum.tile(
+                    [P, B], F32, name="ps%d_%d" % (m, r), tag="Z", bufs=4
+                )
+            wq, ws, o = wqs[(r, g, m)]
             nc.tensor.matmul_mx(
-                out=live[("z", t)][:],
+                out=live[("z", r, m)][:],
                 lhsT=wq[:, o : o + P].bitcast(FP8X4), lhsT_scale=ws[:, o : o + P],
                 rhs=cq[g][:].bitcast(FP8X4), rhs_scale=cs[g][:],
                 start=(g == 0), stop=(g == PASSES - 1),
             )
 
-        def round_of(t):
-            w, q = divmod(t, QS)
-            return w % 2, QS * (w // 2) + q
+        def scalar_a(r):
+            a = epi.tile([P, B], F32, name="a%d" % r, tag="a")
+            nc.scalar.activation(
+                out=a[:], in_=live[("z", r, 1)][:], func=ACT.Tanh, bias=nbt[:, r : r + 1], scale=-1.0
+            )
+            live[("a", r)] = a
 
-        def h_of(r, n):
-            return cn[1 + r // 4][:, :, P * (r % 4) : P * (r % 4 + n)]
+        def scalar_abs(r):
+            u = epi.tile([P, B], F32, name="u%d" % r, tag="u", bufs=4)
+            nc.scalar.activation(
+                out=u[:], in_=live[("z", r, 0)][:], func=ACT.Abs, bias=cst[:, r : r + 1]
+            )
+            live[("u", r)] = u
 
-        def scalar_front(t):
-            m, r = round_of(t)
-            z = live[("z", t)]
-            if m == 0:
-                u = epi.tile([P, B], F32, name="u%d" % r, tag="u")
-                nc.scalar.activation(out=u[:], in_=z[:], func=ACT.Abs, bias=cst[:, r : r + 1])
-                nc.scalar.activation(out=u[:], in_=u[:], func=ACT.Tanh, bias=epsc[:])
-                live[("u", r)] = u
-            else:
-                a = epi.tile([P, B], F32, name="a%d" % r, tag="a")
+        def scalar_tanh(r):
+            u = live[("u", r)]
+            nc.scalar.activation(out=u[:], in_=u[:], func=ACT.Tanh, bias=epsc[:])
+
+        def vector_lin(r):
+            lin = epi.tile([P, B], F32, name="lin%d" % r, tag="lin", bufs=4)
+            nc.vector.tensor_scalar(
+                out=lin[:], in0=live[("u", r)][:], scalar1=c1[:, r : r + 1],
+                scalar2=c0t[:, r : r + 1], op0=ALU.mult, op1=ALU.add,
+            )
+            live[("lin", r)] = lin
+
+        def h_of(r):
+            return cn[1 + r // 4][:, :, P * (r % 4) : P * (r % 4 + 1)]
+
+        def tensor_h(r):
+            dt = psum.tile([P, BT, P], F32, name="dt%d" % r, tag="DT")
+            nc.tensor.matmul(out=dt[:], lhsT=ident_b[:], rhs=h_of(r), start=True, stop=False)
+            nc.tensor.matmul(
+                out=dt[:], lhsT=neg0[:],
+                rhs=brow[:, P * r : P * (r + 1)].unsqueeze(1).to_broadcast([P, BT, P]),
+                start=False, stop=False,
+            )
+            live[("dt", r)] = dt
+
+        def tensor_r(r):
+            rt = psum.tile([P, BT, P], F32, name="rt%d" % r, tag="RT")
+            for i in range(BT):
+                nc.tensor.transpose(
+                    rt[:, i, :], live[("lin", r)][:, P * i : P * (i + 1)], ident_f[:]
+                )
+            live[("rt", r)] = rt
+
+        def tensor_a(r):
+            for i in range(BT):
+                nc.tensor.matmul(
+                    out=live[("dt", r)][:, i, :], lhsT=live[("a", r)][:, P * i : P * (i + 1)],
+                    rhs=ident_f[:], is_transpose=True, start=False, stop=(i == BT - 1),
+                )
+
+        def scalar_decay(r):
+            dec = epi.tile([P, BT, P], F32, name="dec%d" % r, tag="dec")
+            for i in range(BT):
                 nc.scalar.activation(
-                    out=a[:], in_=z[:], func=ACT.Tanh, bias=nbt[:, r : r + 1], scale=-1.0
+                    out=dec[:, i, :], in_=live[("rt", r)][:, i, :], func=ACT.Exp,
+                    scale=cst[:, 64 + i : 65 + i],
                 )
-                live[("a", r)] = a
-
-        def vector_front(t):
-            m, r = round_of(t)
-            if m == 0:
-                lin = epi.tile([P, B], F32, name="lin%d" % r, tag="lin")
-                nc.vector.tensor_scalar(
-                    out=lin[:], in0=live[("u", r)][:], scalar1=c1[:, r : r + 1],
-                    scalar2=c0t[:, r : r + 1], op0=ALU.mult, op1=ALU.add,
-                )
-                live[("lin", r)] = lin
-
-        def tensor_back(t):
-            m, r = round_of(t)
-            if m == 0:
-                rt = psum.tile([P, BT, P], F32, name="rt%d" % r, tag="RT")
-                for i in range(BT):
-                    nc.tensor.transpose(
-                        rt[:, i, :], live[("lin", r)][:, P * i : P * (i + 1)], ident_f[:]
-                    )
-                live[("rt", r)] = rt
-            else:
-                dt = psum.tile([P, BT, P], F32, name="dt%d" % r, tag="DT")
-                nc.tensor.matmul(
-                    out=dt[:], lhsT=ident_b[:], rhs=h_of(r, 1), start=True, stop=False
-                )
-                nc.tensor.matmul(
-                    out=dt[:], lhsT=neg0[:],
-                    rhs=brow[:, P * r : P * (r + 1)].unsqueeze(1).to_broadcast([P, BT, P]),
-                    start=False, stop=False,
-                )
-                for i in range(BT):
-                    nc.tensor.matmul(
-                        out=dt[:, i, :], lhsT=live[("a", r)][:, P * i : P * (i + 1)],
-                        rhs=ident_f[:], is_transpose=True, start=False, stop=(i == BT - 1),
-                    )
-                live[("dt", r)] = dt
-
-        def scalar_decay(t):
-            m, r = round_of(t)
-            if m == 0:
-                dec = epi.tile([P, BT, P], F32, name="dec%d" % r, tag="dec", bufs=6)
-                for i in range(BT):
-                    nc.scalar.activation(
-                        out=dec[:, i, :], in_=live[("rt", r)][:, i, :], func=ACT.Exp,
-                        scale=cst[:, 64 + i : 65 + i],
-                    )
-                live[("dec", r)] = dec
+            live[("dec", r)] = dec
 
         out_v = out.rearrange("(i p) c -> p i c", p=P)
 
-        def vector_blend(t):
-            m, r = round_of(t)
-            if m == 0:
-                return
-            if r % 2 == 0:
+        def vector_mix(r):
+            q = r % 2
+            if q == 0:
                 live["osb"] = epi.tile([P, BT, 2 * P], F32, name="osb%d" % r, tag="osb", bufs=3)
-            osb = live["osb"]
-            mine = osb[:, :, P * (r % 2) : P * (r % 2 + 1)]
+            live[("osb", r)] = live["osb"]
             nc.vector.scalar_tensor_tensor(
-                out=mine, in0=live[("dec", r)][:], scalar=-1.0, in1=live[("dt", r)][:],
-                op0=ALU.add, op1=ALU.mult,
+                out=live["osb"][:, :, P * q : P * (q + 1)], in0=live[("dec", r)][:], scalar=-1.0,
+                in1=live[("dt", r)][:], op0=ALU.add, op1=ALU.mult,
             )
-            if r >= ROUNDS - 2:
-                nc.vector.tensor_tensor(out=mine, in0=mine, in1=h_of(r, 1), op=ALU.add)
-            elif r % 2 == 1:
-                nc.vector.tensor_tensor(out=osb[:], in0=osb[:], in1=h_of(r - 1, 2), op=ALU.add)
-            if r % 2 == 1:
+
+        def vector_add(r):
+            q = r % 2
+            osb = live[("osb", r)]
+            mine = osb[:, :, P * q : P * (q + 1)]
+            nc.vector.tensor_tensor(out=mine, in0=mine, in1=h_of(r), op=ALU.add)
+            if q == 1:
                 nc.sync.dma_start(out=out_v[:, :, P * (r - 1) : P * (r + 1)], in_=osb[:])
 
+        ctx.enter_context(tc.manual_schedule())
+
+        def products(rounds, m, g):
+            for r in rounds:
+                mx_pass(r, m, g)
+
+        head = range(FIRST)
         for g in range(PASSES):
-            unit = [(0, 0, g)]
-            scalar_prep(unit)
-            vector_copy(unit)
-            c_pass(g)
-            quantise(unit)
-            for q in range(QS):
-                mx_pass(q, g)
+            scalar_prep([(0, g)])
+            vector_copies(0, g)
+            c_transpose(g)
+            c_copies(g)
+            quantise(0, g)
+            c_quantise(g)
+            if g >= 1:
+                products(head, 0, g - 1)
+            if g == 2:
+                pst = psum.tile([P, P], BF16, name="pst", tag="DT")
+                nc.tensor.transpose(pst[:], vecs[:], ident_b[:])
+                cst = const.tile([P, P], F32, name="cst")
+                nc.vector.tensor_copy(out=cst[:], in_=pst[:])
+                itau = const.tile([P, 16], F32, name="itau")
+                nc.scalar.activation(out=itau[:], in_=cst[:, 32:48], func=ACT.Exp, scale=-1.0)
+                t1n = const.tile([P, 16], F32, name="t1n")
+                nc.vector.tensor_scalar(
+                    out=t1n[:], in0=itau[:], scalar1=-EPS, scalar2=-1.0, op0=ALU.mult, op1=ALU.add
+                )
+                nk0 = const.tile([P, 16], F32, name="nk0")
+                nc.vector.reciprocal(out=nk0[:], in_=t1n[:])
+                c1 = const.tile([P, 16], F32, name="c1")
+                nc.vector.scalar_tensor_tensor(
+                    out=c1[:], in0=nk0[:], scalar=-1.0, in1=nk0[:], op0=ALU.mult, op1=ALU.mult
+                )
+                nbt = const.tile([P, 16], F32, name="nbt")
+                nc.vector.tensor_scalar(
+                    out=nbt[:], in0=cst[:, 16:32], scalar1=-1.0, scalar2=None, op0=ALU.mult
+                )
+                c0t = const.tile([P, 16], F32, name="c0t")
+                nc.vector.scalar_tensor_tensor(
+                    out=c0t[:], in0=nk0[:], scalar=EPS, in1=itau[:], op0=ALU.mult, op1=ALU.add
+                )
+                nc.vector.tensor_tensor(out=c0t[:], in0=c0t[:], in1=nk0[:], op=ALU.mult)
+                epsc = const.tile([P, 1], F32, name="epsc")
+                nc.vector.tensor_scalar(
+                    out=epsc[:], in0=itau[:, 0:1], scalar1=0.0, scalar2=EPS, op0=ALU.mult, op1=ALU.add
+                )
+        products(head, 0, PASSES - 1)
 
-        pst = psum.tile([P, P], BF16, name="pst", tag="DT")
-        nc.tensor.transpose(pst[:], vecs[:], ident_b[:])
-        cst = const.tile([P, P], F32, name="cst")
-        nc.vector.tensor_copy(out=cst[:], in_=pst[:])
-        itau = const.tile([P, 16], F32, name="itau")
-        nc.scalar.activation(out=itau[:], in_=cst[:, 32:48], func=ACT.Exp, scale=-1.0)
-        t1n = const.tile([P, 16], F32, name="t1n")
-        nc.vector.tensor_scalar(
-            out=t1n[:], in0=itau[:], scalar1=-EPS, scalar2=-1.0, op0=ALU.mult, op1=ALU.add
-        )
-        nk0 = const.tile([P, 16], F32, name="nk0")
-        nc.vector.reciprocal(out=nk0[:], in_=t1n[:])
-        c1 = const.tile([P, 16], F32, name="c1")
-        nc.vector.scalar_tensor_tensor(
-            out=c1[:], in0=nk0[:], scalar=-1.0, in1=nk0[:], op0=ALU.mult, op1=ALU.mult
-        )
-        nbt = const.tile([P, 16], F32, name="nbt")
-        nc.vector.tensor_scalar(
-            out=nbt[:], in0=cst[:, 16:32], scalar1=-1.0, scalar2=None, op0=ALU.mult
-        )
-        c0t = const.tile([P, 16], F32, name="c0t")
-        nc.vector.scalar_tensor_tensor(
-            out=c0t[:], in0=nk0[:], scalar=EPS, in1=itau[:], op0=ALU.mult, op1=ALU.add
-        )
-        nc.vector.tensor_tensor(out=c0t[:], in0=c0t[:], in1=nk0[:], op=ALU.mult)
-        epsc = const.tile([P, 1], F32, name="epsc")
-        nc.vector.tensor_scalar(
-            out=epsc[:], in0=itau[:, 0:1], scalar1=0.0, scalar2=EPS, op0=ALU.mult, op1=ALU.add
-        )
+        for r in head:
+            scalar_abs(r)
+        for g in range(PASSES):
+            scalar_prep([(1, g)])
+            if g < FIRST:
+                scalar_tanh(g)
+            vector_copies(1, g)
+            if g >= 1:
+                vector_lin(g - 1)
+            quantise(1, g)
+            products(head, 1, g)
 
-        stream = [
-            (w, pt, g)
-            for w in range(1, GROUPS)
-            for pt in range(len(parts_of(w)))
-            for g in range(PASSES)
-        ]
-        sets = [[] for t in range(STEPS + 1)]
-        total = (GROUPS - 1) * PASSES * SLAB
+        stream = [(w, g) for w in range(2, len(GROUPS)) for g in range(PASSES)]
+        sets = [[] for b in range(ROUNDS + 4)]
+        total = sum(columns_of(w) for w, g in stream)
         pos = 0
         done = 0
-        for t in range(STEPS - 2):
-            target = total * (t + 2) / (STEPS - 1)
-            while pos < len(stream):
-                w, pt, g = stream[pos]
-                c0, n = parts_of(w)[pt]
-                if done >= target and QS * w + c0 // P - 2 > t:
-                    break
-                sets[t].append(stream[pos])
-                done += n
+        PREP = ROUNDS - 2
+        for b in range(PREP):
+            target = total * (b + 1) / PREP
+            while pos < len(stream) and (done < target or GROUPS[stream[pos][0]][0][1] // P <= b + 2):
+                sets[b].append(stream[pos])
+                done += columns_of(stream[pos][0])
                 pos += 1
         assert pos == len(stream)
 
         scalar_prep(sets[0])
-        for t in range(STEPS + 1):
-            if t >= 1:
-                tensor_back(t - 1)
-            if QS <= t + 1 < STEPS:
+        tensor_h(0)
+        for b in range(ROUNDS + 1):
+            now = b < ROUNDS
+            more = FIRST <= b + 1 < ROUNDS
+            nxt = sets[b + 1]
+            kn = (len(nxt) + 1) // 2
+            units = sets[b]
+            k = (len(units) + 1) // 2
+            if more:
                 for g in range(PASSES):
-                    mx_pass(t + 1, g)
-            if t < STEPS:
-                scalar_front(t)
-            if t >= 1:
-                scalar_decay(t - 1)
-            if t < STEPS:
-                scalar_prep(sets[t + 1])
-            vector_copy(sets[t])
-            quantise(sets[t])
-            if t < STEPS:
-                vector_front(t)
-            if t >= 1:
-                vector_blend(t - 1)
+                    mx_pass(b + 1, 0, g)
+            if now:
+                scalar_a(b)
+            scalar_prep(nxt[:kn])
+            if more:
+                scalar_abs(b + 1)
+            if FIRST <= b < ROUNDS:
+                vector_lin(b)
+            if now:
+                tensor_r(b)
+            if now:
+                tensor_a(b)
+            if more:
+                for g in range(PASSES):
+                    mx_pass(b + 1, 1, g)
+            if b + 1 < ROUNDS:
+                tensor_h(b + 1)
+            if now:
+                scalar_decay(b)
+            scalar_prep(nxt[kn:])
+            if more:
+                scalar_tanh(b + 1)
+            for unit in units[:k]:
+                vector_copies(*unit)
+            if b >= 1 and b - 1 < ROUNDS:
+                vector_mix(b - 1)
+            for unit in units[:k]:
+                quantise(*unit)
+            for unit in units[k:]:
+                vector_copies(*unit)
+            if b >= 1 and b - 1 < ROUNDS:
+                vector_add(b - 1)
+            for unit in units[k:]:
+                quantise(*unit)

@@ -28,8 +28,8 @@ FIRST = SLAB // P
 
 def group_list():
     groups = [((0, 0, SLAB),), ((1, 0, SLAB),)]
-    groups += [((0, P * r, 2 * P), (1, P * r, 2 * P)) for r in range(FIRST, ROUNDS - 2, 2)]
-    groups += [((0, P * r, P), (1, P * r, P)) for r in range(ROUNDS - 2, ROUNDS)]
+    groups += [((0, P * r, 2 * P), (1, P * r, 2 * P)) for r in range(FIRST, ROUNDS - 4, 2)]
+    groups += [((0, P * r, P), (1, P * r, P)) for r in range(ROUNDS - 4, ROUNDS)]
     return groups
 
 
@@ -47,8 +47,8 @@ def scalar_columns(w, g):
     if w == 0:
         return 3 * n // 4
     if w == 1:
-        return n // 2 if g >= 2 else 0
-    return n // 2 if g < 4 else 0
+        return n // 2 if g >= 3 else 0
+    return (n // 2 if g < 4 or w == 2 or w >= len(GROUPS) - 4 else 0)
 
 
 def tile_ltccell_kernel(
@@ -397,36 +397,36 @@ def tile_ltccell_kernel(
             if more:
                 for g in range(PASSES):
                     mx_pass(b + 1, 0, g)
+            if more:
+                for g in range(PASSES):
+                    mx_pass(b + 1, 1, g)
             if now:
                 scalar_a(b)
             scalar_prep(nxt[:kn])
             if more:
                 scalar_abs(b + 1)
+            scalar_prep(nxt[kn:])
+            if more:
+                scalar_tanh(b + 1)
+            for unit in units[:k]:
+                vector_copies(*unit)
             if FIRST <= b < ROUNDS:
                 vector_lin(b)
             if now:
                 tensor_r(b)
             if now:
                 tensor_a(b)
-            if more:
-                for g in range(PASSES):
-                    mx_pass(b + 1, 1, g)
             if b + 1 < ROUNDS:
                 tensor_h(b + 1)
             if now:
                 scalar_decay(b)
-            scalar_prep(nxt[kn:])
-            if more:
-                scalar_tanh(b + 1)
-            for unit in units[:k]:
+            for unit in units[k:]:
                 vector_copies(*unit)
+            for unit in units[:k]:
+                quantise(*unit)
             if b >= 1 and b - 1 < ROUNDS:
                 vector_mix(b - 1)
-            for unit in units[:k]:
-                quantise(*unit)
             for unit in units[k:]:
-                vector_copies(*unit)
+                quantise(*unit)
             if b >= 1 and b - 1 < ROUNDS:
                 vector_add(b - 1)
-            for unit in units[k:]:
-                quantise(*unit)

@@ -23,19 +23,28 @@ EPS = 1e-6
 FLOPS = 2 * 2 * B * K * H
 
 SLAB = 512
-RAW_BUFS = 16
-FIRST = SLAB // P
+RAW_BUFS = 14
+LEAD = SLAB // P
+
 
 def group_list():
-    groups = [((0, 0, SLAB),), ((1, 0, SLAB),)]
-    groups += [((0, P * r, 2 * P), (1, P * r, 2 * P)) for r in range(FIRST, ROUNDS - 4, 2)]
-    groups += [((0, P * r, P), (1, P * r, P)) for r in range(ROUNDS - 4, ROUNDS)]
+    groups = [((0, 0, SLAB),), ((1, 0, SLAB),), ((0, SLAB, SLAB),)]
+    groups += [
+        ((1, P * r, 2 * P), (0, P * (r + LEAD), 2 * P)) for r in range(LEAD, ROUNDS - LEAD, 2)
+    ]
+    groups += [((1, P * r, 2 * P),) for r in range(ROUNDS - LEAD, ROUNDS - 2, 2)]
+    groups += [((1, P * r, P),) for r in range(ROUNDS - 2, ROUNDS)]
     return groups
 
 
 GROUPS = group_list()
-GRP_BUFS = {SLAB: 6, 2 * P: 6}
-WQ_BUFS = {SLAB: 3, 2 * P: 2}
+GRP_BUFS = {SLAB: 5, 2 * P: 5, P: 10}
+WQ_BUFS = {SLAB: 3, 2 * P: 1, P: 2}
+
+
+def first_round(w):
+    m, c0, n = GROUPS[w][0]
+    return c0 // P - (0 if m else LEAD)
 
 
 def columns_of(w):
@@ -47,8 +56,10 @@ def scalar_columns(w, g):
     if w == 0:
         return 3 * n // 4
     if w == 1:
-        return n // 2 if g >= 3 else 0
-    return (n // 2 if g < 4 or w == 2 or w >= len(GROUPS) - 4 else 0)
+        return n // 2 if g == 0 or g >= 3 else 0
+    if w == 2:
+        return n // 2 if g < 3 else 0
+    return n // 2 if g < 4 else 0
 
 
 def tile_ltccell_kernel(
@@ -96,8 +107,10 @@ def tile_ltccell_kernel(
             nc.sync.dma_start(out=cng[:], in_=src.rearrange("(i p) k -> p i k", p=P))
             cn.append(cng)
 
-        chunks = [(0, g, m) for m in range(2) for g in range(PASSES)]
-        chunks += [(c0, g, m) for c0 in range(SLAB, H, SLAB) for g in range(PASSES) for m in range(2)]
+        chunks = [(c0, g, m) for c0, m in ((0, 0), (0, 1), (SLAB, 0)) for g in range(PASSES)]
+        for c0 in range(SLAB, H, SLAB):
+            for g in range(PASSES):
+                chunks += [(c, g, m) for c, m in ((c0, 1), (c0 + SLAB, 0)) if c < H]
         raws = {}
         ring = {"next": 0, "free": RAW_BUFS}
 
@@ -247,7 +260,7 @@ def tile_ltccell_kernel(
             nc.scalar.activation(out=u[:], in_=u[:], func=ACT.Tanh, bias=epsc[:])
 
         def vector_lin(r):
-            lin = epi.tile([P, B], F32, name="lin%d" % r, tag="lin", bufs=4)
+            lin = epi.tile([P, B], F32, name="lin%d" % r, tag="lin", bufs=3)
             nc.vector.tensor_scalar(
                 out=lin[:], in0=live[("u", r)][:], scalar1=c1[:, r : r + 1],
                 scalar2=c0t[:, r : r + 1], op0=ALU.mult, op1=ALU.add,
@@ -283,7 +296,7 @@ def tile_ltccell_kernel(
                 )
 
         def scalar_decay(r):
-            dec = epi.tile([P, BT, P], F32, name="dec%d" % r, tag="dec")
+            dec = epi.tile([P, BT, P], F32, name="dec%d" % r, tag="dec", bufs=6)
             for i in range(BT):
                 nc.scalar.activation(
                     out=dec[:, i, :], in_=live[("rt", r)][:, i, :], func=ACT.Exp,
@@ -293,10 +306,25 @@ def tile_ltccell_kernel(
 
         out_v = out.rearrange("(i p) c -> p i c", p=P)
 
+        def parts_of(r):
+            return (slice(0, 2), slice(2, 4)) if r == ROUNDS - 1 else (slice(0, BT),)
+
         def vector_mix(r):
             q = r % 2
+            if r >= ROUNDS - 2:
+                live[("osb", r)] = []
+                for n, i in enumerate(parts_of(r)):
+                    o = epi.tile(
+                        [P, i.stop - i.start, P], F32, name="ose%d_%d" % (r, n), tag="ose", bufs=3
+                    )
+                    live[("osb", r)].append(o)
+                    nc.vector.scalar_tensor_tensor(
+                        out=o[:], in0=live[("dec", r)][:, i, :], scalar=-1.0,
+                        in1=live[("dt", r)][:, i, :], op0=ALU.add, op1=ALU.mult,
+                    )
+                return
             if q == 0:
-                live["osb"] = epi.tile([P, BT, 2 * P], F32, name="osb%d" % r, tag="osb", bufs=3)
+                live["osb"] = epi.tile([P, BT, 2 * P], F32, name="osb%d" % r, tag="osb", bufs=2)
             live[("osb", r)] = live["osb"]
             nc.vector.scalar_tensor_tensor(
                 out=live["osb"][:, :, P * q : P * (q + 1)], in0=live[("dec", r)][:], scalar=-1.0,
@@ -306,6 +334,11 @@ def tile_ltccell_kernel(
         def vector_add(r):
             q = r % 2
             osb = live[("osb", r)]
+            if r >= ROUNDS - 2:
+                for o, i in zip(osb, parts_of(r)):
+                    nc.vector.tensor_tensor(out=o[:], in0=o[:], in1=h_of(r)[:, i, :], op=ALU.add)
+                    nc.sync.dma_start(out=out_v[:, i, P * r : P * (r + 1)], in_=o[:])
+                return
             mine = osb[:, :, P * q : P * (q + 1)]
             nc.vector.tensor_tensor(out=mine, in0=mine, in1=h_of(r), op=ALU.add)
             if q == 1:
@@ -317,7 +350,7 @@ def tile_ltccell_kernel(
             for r in rounds:
                 mx_pass(r, m, g)
 
-        head = range(FIRST)
+        head = range(LEAD)
         for g in range(PASSES):
             scalar_prep([(0, g)])
             vector_copies(0, g)
@@ -327,13 +360,15 @@ def tile_ltccell_kernel(
             c_quantise(g)
             if g >= 1:
                 products(head, 0, g - 1)
-            if g == 2:
+            if g == 0:
                 pst = psum.tile([P, P], BF16, name="pst", tag="DT")
                 nc.tensor.transpose(pst[:], vecs[:], ident_b[:])
                 cst = const.tile([P, P], F32, name="cst")
                 nc.vector.tensor_copy(out=cst[:], in_=pst[:])
+            if g == 1:
                 itau = const.tile([P, 16], F32, name="itau")
                 nc.scalar.activation(out=itau[:], in_=cst[:, 32:48], func=ACT.Exp, scale=-1.0)
+            if g == 2:
                 t1n = const.tile([P, 16], F32, name="t1n")
                 nc.vector.tensor_scalar(
                     out=t1n[:], in0=itau[:], scalar1=-EPS, scalar2=-1.0, op0=ALU.mult, op1=ALU.add
@@ -359,19 +394,44 @@ def tile_ltccell_kernel(
                 )
         products(head, 0, PASSES - 1)
 
+        scalar_prep([(1, 0)])
         for r in head:
             scalar_abs(r)
         for g in range(PASSES):
-            scalar_prep([(1, g)])
-            if g < FIRST:
+            if g >= 1:
+                scalar_prep([(1, g)])
+            if g < LEAD:
                 scalar_tanh(g)
             vector_copies(1, g)
             if g >= 1:
                 vector_lin(g - 1)
             quantise(1, g)
             products(head, 1, g)
+            if 1 <= g <= 2:
+                tensor_r(g - 1)
 
-        stream = [(w, g) for w in range(2, len(GROUPS)) for g in range(PASSES)]
+        for g in range(PASSES):
+            scalar_prep([(2, g)])
+            if g == 0:
+                scalar_decay(0)
+                tensor_r(2)
+            if g == 1:
+                scalar_decay(1)
+                tensor_r(3)
+            if g == 2:
+                scalar_a(0)
+                scalar_decay(2)
+            if g == 3:
+                scalar_decay(3)
+            vector_copies(2, g)
+            if g >= 1:
+                quantise(2, g - 1)
+                mx_pass(LEAD, 0, g - 1)
+        quantise(2, PASSES - 1)
+        mx_pass(LEAD, 0, PASSES - 1)
+        tensor_h(0)
+
+        stream = [(w, g) for w in range(3, len(GROUPS)) for g in range(PASSES)]
         sets = [[] for b in range(ROUNDS + 4)]
         total = sum(columns_of(w) for w, g in stream)
         pos = 0
@@ -379,54 +439,55 @@ def tile_ltccell_kernel(
         PREP = ROUNDS - 2
         for b in range(PREP):
             target = total * (b + 1) / PREP
-            while pos < len(stream) and (done < target or GROUPS[stream[pos][0]][0][1] // P <= b + 2):
+            while pos < len(stream) and (done < target or first_round(stream[pos][0]) <= b + 2):
                 sets[b].append(stream[pos])
                 done += columns_of(stream[pos][0])
                 pos += 1
         assert pos == len(stream)
 
         scalar_prep(sets[0])
-        tensor_h(0)
+        scalar_abs(LEAD)
+        scalar_tanh(LEAD)
         for b in range(ROUNDS + 1):
             now = b < ROUNDS
-            more = FIRST <= b + 1 < ROUNDS
-            nxt = sets[b + 1]
-            kn = (len(nxt) + 1) // 2
+            f = b + LEAD
             units = sets[b]
             k = (len(units) + 1) // 2
-            if more:
+            nxt = sets[b + 1]
+            kn = (len(nxt) + 1) // 2
+            if f + 1 < ROUNDS:
                 for g in range(PASSES):
-                    mx_pass(b + 1, 0, g)
-            if more:
+                    mx_pass(f + 1, 0, g)
+            if LEAD <= b + 1 < ROUNDS:
                 for g in range(PASSES):
                     mx_pass(b + 1, 1, g)
-            if now:
+            if 1 <= b < ROUNDS:
                 scalar_a(b)
             scalar_prep(nxt[:kn])
-            if more:
-                scalar_abs(b + 1)
+            if f + 1 < ROUNDS:
+                scalar_abs(f + 1)
             scalar_prep(nxt[kn:])
-            if more:
-                scalar_tanh(b + 1)
+            if f + 1 < ROUNDS:
+                scalar_tanh(f + 1)
             for unit in units[:k]:
                 vector_copies(*unit)
-            if FIRST <= b < ROUNDS:
-                vector_lin(b)
-            if now:
-                tensor_r(b)
+            for unit in units[k:]:
+                vector_copies(*unit)
+            for unit in units[:k]:
+                quantise(*unit)
+            if f < ROUNDS:
+                vector_lin(f)
+            if f < ROUNDS:
+                tensor_r(f)
             if now:
                 tensor_a(b)
             if b + 1 < ROUNDS:
                 tensor_h(b + 1)
-            if now:
-                scalar_decay(b)
-            for unit in units[k:]:
-                vector_copies(*unit)
-            for unit in units[:k]:
-                quantise(*unit)
-            if b >= 1 and b - 1 < ROUNDS:
+            if f < ROUNDS:
+                scalar_decay(f)
+            if b >= 1:
                 vector_mix(b - 1)
             for unit in units[k:]:
                 quantise(*unit)
-            if b >= 1 and b - 1 < ROUNDS:
+            if b >= 1:
                 vector_add(b - 1)

@@ -23,43 +23,32 @@ EPS = 1e-6
 FLOPS = 2 * 2 * B * K * H
 
 SLAB = 512
-RAW_BUFS = 14
-LEAD = SLAB // P
+RAW_BUFS = 16
 
 
 def group_list():
-    groups = [((0, 0, SLAB),), ((1, 0, SLAB),), ((0, SLAB, SLAB),)]
-    groups += [
-        ((1, P * r, 2 * P), (0, P * (r + LEAD), 2 * P)) for r in range(LEAD, ROUNDS - LEAD, 2)
-    ]
-    groups += [((1, P * r, 2 * P),) for r in range(ROUNDS - LEAD, ROUNDS - 2, 2)]
-    groups += [((1, P * r, P),) for r in range(ROUNDS - 2, ROUNDS)]
-    return groups
+    groups = [(m, c0, SLAB) for c0 in range(0, H, SLAB) for m in range(2)][:-1]
+    return groups + [(1, H - SLAB, 2 * P), (1, H - 2 * P, 2 * P)]
 
 
 GROUPS = group_list()
-GRP_BUFS = {SLAB: 5, 2 * P: 5, P: 10}
-WQ_BUFS = {SLAB: 3, 2 * P: 1, P: 2}
+GRP_BUFS = {SLAB: 6, 2 * P: 8, P: 6}
+WQ_BUFS = {SLAB: 4, 2 * P: 4, P: 4}
+AHEAD = 2
 
 
-def first_round(w):
-    m, c0, n = GROUPS[w][0]
-    return c0 // P - (0 if m else LEAD)
-
-
-def columns_of(w):
-    return sum(n for m, c0, n in GROUPS[w])
+def rounds_of(w):
+    m, c0, n = GROUPS[w]
+    return range(c0 // P, (c0 + n) // P)
 
 
 def scalar_columns(w, g):
-    n = columns_of(w)
+    n = GROUPS[w][2]
     if w == 0:
         return 3 * n // 4
     if w == 1:
-        return n // 2 if g == 0 or g >= 3 else 0
-    if w == 2:
-        return n // 2 if g < 3 else 0
-    return n // 2 if g < 4 else 0
+        return n // 2 if g % 2 else n // 4
+    return n // 4 if g in (0, 2) else n // 2 if w < 7 else n // 4
 
 
 def tile_ltccell_kernel(
@@ -101,16 +90,16 @@ def tile_ltccell_kernel(
 
         cn = []
 
-        def load_c(g):
-            src = x if g == 0 else h[:, K_PASS * (g - 1) : K_PASS * g]
-            cng = const.tile([P, BT, K_PASS], BF16, name="cn%d" % g)
-            nc.sync.dma_start(out=cng[:], in_=src.rearrange("(i p) k -> p i k", p=P))
-            cn.append(cng)
+        def load_c(src, passes):
+            n = K_PASS * passes
+            tile = const.tile([P, BT, n], BF16, name="cn%d" % len(cn))
+            nc.sync.dma_start(out=tile[:], in_=src.rearrange("(i p) k -> p i k", p=P))
+            for g in range(passes):
+                cn.append(tile[:, :, K_PASS * g : K_PASS * (g + 1)])
 
-        chunks = [(c0, g, m) for c0, m in ((0, 0), (0, 1), (SLAB, 0)) for g in range(PASSES)]
-        for c0 in range(SLAB, H, SLAB):
-            for g in range(PASSES):
-                chunks += [(c, g, m) for c, m in ((c0, 1), (c0 + SLAB, 0)) if c < H]
+        chunks = [
+            (c0, g, m) for c0 in range(0, H, SLAB) for m in range(2) for g in range(PASSES)
+        ]
         raws = {}
         ring = {"next": 0, "free": RAW_BUFS}
 
@@ -127,8 +116,12 @@ def tile_ltccell_kernel(
                     ),
                 )
                 raws[(c0 // SLAB, g, m)] = raw
-                if ring["next"] < PASSES:
-                    load_c(g)
+                if ring["next"] == 0:
+                    load_c(x, 1)
+                if ring["next"] == 1:
+                    load_c(h[:, : H // 2], 2)
+                if ring["next"] == 3:
+                    load_c(h[:, H // 2 :], 2)
                 ring["free"] -= 1
                 ring["next"] += 1
 
@@ -140,10 +133,11 @@ def tile_ltccell_kernel(
         cgs = {}
 
         def c_transpose(g):
-            cnf = cn[g][:].bitcast(F32).rearrange("p i (q u) -> p i u q", u=2)
+            cnf = cn[g].bitcast(F32).rearrange("p i (q u) -> p i u q", u=2)
             for half in range(2):
                 xt = psum.tile(
-                    [P, 2, 2, P], F32, name="xt%d_%d" % (g, half), tag=("RT", "DT")[half]
+                    [P, 2, 2, P], F32, name="xt%d_%d" % (g, half), tag=("RT", "DT")[half],
+                    bufs=1,
                 )
                 for il in range(2):
                     for u in range(2):
@@ -176,62 +170,51 @@ def tile_ltccell_kernel(
         live = {}
 
         def regroup(w, g, lo, hi, engine_copy):
-            at = 0
-            for m, c0, n in GROUPS[w]:
-                a = max(lo, at)
-                b = min(hi, at + n)
-                if a < b:
-                    o = c0 % SLAB + a - at
-                    engine_copy(
-                        out=grps[(w, g)][:, a:b, :].rearrange("p (c i) t -> p c t i", i=4),
-                        in_=raws[(c0 // SLAB, g, m)][:, :, o : o + b - a].rearrange(
-                            "p t (c i) -> p c t i", i=4
-                        ),
-                    )
-                at += n
+            m, c0, n = GROUPS[w]
+            o = c0 % SLAB
+            engine_copy(
+                out=grps[(w, g)][:, lo:hi, :].rearrange("p (c i) t -> p c t i", i=4),
+                in_=raws[(c0 // SLAB, g, m)][:, :, o + lo : o + hi].rearrange(
+                    "p t (c i) -> p c t i", i=4
+                ),
+            )
 
-        def scalar_prep(units):
-            for w, g in units:
-                n = columns_of(w)
-                grps[(w, g)] = grpp.tile(
-                    [P, n, PACK], BF16, name="grp%d_%d" % (w, g), tag="grp%d" % n, align_bytes=64,
-                    bufs=GRP_BUFS[n],
-                )
-                for a in range(n - scalar_columns(w, g), n, 2 * P):
-                    regroup(w, g, a, min(n, a + 2 * P), nc.scalar.copy)
+        def scalar_prep(w, g):
+            n = GROUPS[w][2]
+            grps[(w, g)] = grpp.tile(
+                [P, n, PACK], BF16, name="grp%d_%d" % (w, g), tag="grp%d" % n, align_bytes=64,
+                bufs=GRP_BUFS[n],
+            )
+            for a in range(n - scalar_columns(w, g), n, 2 * P):
+                regroup(w, g, a, min(n, a + 2 * P), nc.scalar.copy)
 
         def vector_copies(w, g):
-            n = columns_of(w)
-            regroup(w, g, 0, n - scalar_columns(w, g), nc.vector.tensor_copy)
-            for m, c0, size in GROUPS[w]:
-                if (c0 + size) % SLAB == 0:
-                    ring["free"] += 1
+            m, c0, n = GROUPS[w]
+            if scalar_columns(w, g) < n:
+                regroup(w, g, 0, n - scalar_columns(w, g), nc.vector.tensor_copy)
+            if (c0 + n) % SLAB == 0:
+                ring["free"] += 1
             load_more()
 
         def quantise(w, g):
-            n = columns_of(w)
+            m, c0, n = GROUPS[w]
             wq = wqp.tile(
-                [P, n], U32, name="wq%d_%d" % (w, g), tag="wq%d_%d" % (n, g), align_bytes=64,
-                bufs=WQ_BUFS[n],
+                [P, n], U32, name="wq%d_%d" % (w, g), tag="wq%d" % n, align_bytes=64, bufs=WQ_BUFS[n]
             )
             ws = wqp.tile(
-                [P, n], U8, name="ws%d_%d" % (w, g), tag="ws%d_%d" % (n, g), align_bytes=64,
-                bufs=WQ_BUFS[n],
+                [P, n], U8, name="ws%d_%d" % (w, g), tag="ws%d" % n, align_bytes=64, bufs=WQ_BUFS[n]
             )
             nc.vector.quantize_mx(
                 out=wq[:].bitcast(FP8X4), scales=ws[:],
                 in_=grps[(w, g)][:].rearrange("p w t -> p (w t)"),
             )
-            at = 0
-            for m, c0, size in GROUPS[w]:
-                for i in range(size // P):
-                    wqs[(c0 // P + i, g, m)] = (wq, ws, at + P * i)
-                at += size
+            for i, r in enumerate(rounds_of(w)):
+                wqs[(r, g, m)] = (wq, ws, P * i)
 
         def mx_pass(r, m, g):
             if g == 0:
                 live[("z", r, m)] = psum.tile(
-                    [P, B], F32, name="ps%d_%d" % (m, r), tag="Z", bufs=4
+                    [P, B], F32, name="ps%d_%d" % (m, r), tag="Z", bufs=6
                 )
             wq, ws, o = wqs[(r, g, m)]
             nc.tensor.matmul_mx(
@@ -242,14 +225,14 @@ def tile_ltccell_kernel(
             )
 
         def scalar_a(r):
-            a = epi.tile([P, B], F32, name="a%d" % r, tag="a")
+            a = epi.tile([P, B], F32, name="a%d" % r, tag="a", bufs=6)
             nc.scalar.activation(
                 out=a[:], in_=live[("z", r, 1)][:], func=ACT.Tanh, bias=nbt[:, r : r + 1], scale=-1.0
             )
             live[("a", r)] = a
 
         def scalar_abs(r):
-            u = epi.tile([P, B], F32, name="u%d" % r, tag="u", bufs=4)
+            u = epi.tile([P, B], F32, name="u%d" % r, tag="u", bufs=6)
             nc.scalar.activation(
                 out=u[:], in_=live[("z", r, 0)][:], func=ACT.Abs, bias=cst[:, r : r + 1]
             )
@@ -260,7 +243,7 @@ def tile_ltccell_kernel(
             nc.scalar.activation(out=u[:], in_=u[:], func=ACT.Tanh, bias=epsc[:])
 
         def vector_lin(r):
-            lin = epi.tile([P, B], F32, name="lin%d" % r, tag="lin", bufs=3)
+            lin = epi.tile([P, B], F32, name="lin%d" % r, tag="lin")
             nc.vector.tensor_scalar(
                 out=lin[:], in0=live[("u", r)][:], scalar1=c1[:, r : r + 1],
                 scalar2=c0t[:, r : r + 1], op0=ALU.mult, op1=ALU.add,
@@ -271,7 +254,7 @@ def tile_ltccell_kernel(
             return cn[1 + r // 4][:, :, P * (r % 4) : P * (r % 4 + 1)]
 
         def tensor_h(r):
-            dt = psum.tile([P, BT, P], F32, name="dt%d" % r, tag="DT")
+            dt = psum.tile([P, BT, P], F32, name="dt%d" % r, tag="DT", bufs=1)
             nc.tensor.matmul(out=dt[:], lhsT=ident_b[:], rhs=h_of(r), start=True, stop=False)
             nc.tensor.matmul(
                 out=dt[:], lhsT=neg0[:],
@@ -281,7 +264,7 @@ def tile_ltccell_kernel(
             live[("dt", r)] = dt
 
         def tensor_r(r):
-            rt = psum.tile([P, BT, P], F32, name="rt%d" % r, tag="RT")
+            rt = psum.tile([P, BT, P], F32, name="rt%d" % r, tag="RT", bufs=1)
             for i in range(BT):
                 nc.tensor.transpose(
                     rt[:, i, :], live[("lin", r)][:, P * i : P * (i + 1)], ident_f[:]
@@ -296,7 +279,7 @@ def tile_ltccell_kernel(
                 )
 
         def scalar_decay(r):
-            dec = epi.tile([P, BT, P], F32, name="dec%d" % r, tag="dec", bufs=6)
+            dec = epi.tile([P, BT, P], F32, name="dec%d" % r, tag="dec", bufs=4)
             for i in range(BT):
                 nc.scalar.activation(
                     out=dec[:, i, :], in_=live[("rt", r)][:, i, :], func=ACT.Exp,
@@ -324,7 +307,7 @@ def tile_ltccell_kernel(
                     )
                 return
             if q == 0:
-                live["osb"] = epi.tile([P, BT, 2 * P], F32, name="osb%d" % r, tag="osb", bufs=2)
+                live["osb"] = epi.tile([P, BT, 2 * P], F32, name="osb%d" % r, tag="osb", bufs=3)
             live[("osb", r)] = live["osb"]
             nc.vector.scalar_tensor_tensor(
                 out=live["osb"][:, :, P * q : P * (q + 1)], in0=live[("dec", r)][:], scalar=-1.0,
@@ -346,22 +329,26 @@ def tile_ltccell_kernel(
 
         ctx.enter_context(tc.manual_schedule())
 
-        def products(rounds, m, g):
-            for r in rounds:
-                mx_pass(r, m, g)
+        def products(w, g):
+            for r in rounds_of(w):
+                mx_pass(r, GROUPS[w][0], g)
 
-        head = range(LEAD)
+        def leave(w, n):
+            if n < len(rounds_of(w)):
+                (scalar_a if GROUPS[w][0] else scalar_abs)(rounds_of(w)[n])
+
+        units = [(w, g) for w in range(1, len(GROUPS)) for g in range(PASSES)]
         for g in range(PASSES):
-            scalar_prep([(0, g)])
+            scalar_prep(0, g)
             vector_copies(0, g)
             c_transpose(g)
             c_copies(g)
             quantise(0, g)
             c_quantise(g)
             if g >= 1:
-                products(head, 0, g - 1)
+                products(0, g - 1)
             if g == 0:
-                pst = psum.tile([P, P], BF16, name="pst", tag="DT")
+                pst = psum.tile([P, P], BF16, name="pst", tag="DT", bufs=1)
                 nc.tensor.transpose(pst[:], vecs[:], ident_b[:])
                 cst = const.tile([P, P], F32, name="cst")
                 nc.vector.tensor_copy(out=cst[:], in_=pst[:])
@@ -392,102 +379,112 @@ def tile_ltccell_kernel(
                 nc.vector.tensor_scalar(
                     out=epsc[:], in0=itau[:, 0:1], scalar1=0.0, scalar2=EPS, op0=ALU.mult, op1=ALU.add
                 )
-        products(head, 0, PASSES - 1)
 
-        scalar_prep([(1, 0)])
-        for r in head:
-            scalar_abs(r)
-        for g in range(PASSES):
-            if g >= 1:
-                scalar_prep([(1, g)])
-            if g < LEAD:
-                scalar_tanh(g)
-            vector_copies(1, g)
-            if g >= 1:
-                vector_lin(g - 1)
-            quantise(1, g)
-            products(head, 1, g)
-            if 1 <= g <= 2:
-                tensor_r(g - 1)
+        def at(fn, r):
+            if 0 <= r < ROUNDS:
+                fn(r)
 
-        for g in range(PASSES):
-            scalar_prep([(2, g)])
-            if g == 0:
-                scalar_decay(0)
-                tensor_r(2)
-            if g == 1:
-                scalar_decay(1)
-                tensor_r(3)
-            if g == 2:
-                scalar_a(0)
-                scalar_decay(2)
-            if g == 3:
-                scalar_decay(3)
-            vector_copies(2, g)
-            if g >= 1:
-                quantise(2, g - 1)
-                mx_pass(LEAD, 0, g - 1)
-        quantise(2, PASSES - 1)
-        mx_pass(LEAD, 0, PASSES - 1)
-        tensor_h(0)
-
-        stream = [(w, g) for w in range(3, len(GROUPS)) for g in range(PASSES)]
-        sets = [[] for b in range(ROUNDS + 4)]
-        total = sum(columns_of(w) for w, g in stream)
-        pos = 0
-        done = 0
-        PREP = ROUNDS - 2
-        for b in range(PREP):
-            target = total * (b + 1) / PREP
-            while pos < len(stream) and (done < target or first_round(stream[pos][0]) <= b + 2):
-                sets[b].append(stream[pos])
-                done += columns_of(stream[pos][0])
-                pos += 1
-        assert pos == len(stream)
-
-        scalar_prep(sets[0])
-        scalar_abs(LEAD)
-        scalar_tanh(LEAD)
-        for b in range(ROUNDS + 1):
-            now = b < ROUNDS
-            f = b + LEAD
-            units = sets[b]
-            k = (len(units) + 1) // 2
-            nxt = sets[b + 1]
-            kn = (len(nxt) + 1) // 2
-            if f + 1 < ROUNDS:
-                for g in range(PASSES):
-                    mx_pass(f + 1, 0, g)
-            if LEAD <= b + 1 < ROUNDS:
-                for g in range(PASSES):
-                    mx_pass(b + 1, 1, g)
-            if 1 <= b < ROUNDS:
-                scalar_a(b)
-            scalar_prep(nxt[:kn])
-            if f + 1 < ROUNDS:
-                scalar_abs(f + 1)
-            scalar_prep(nxt[kn:])
-            if f + 1 < ROUNDS:
-                scalar_tanh(f + 1)
-            for unit in units[:k]:
-                vector_copies(*unit)
-            for unit in units[k:]:
-                vector_copies(*unit)
-            for unit in units[:k]:
-                quantise(*unit)
-            if f < ROUNDS:
-                vector_lin(f)
-            if f < ROUNDS:
-                tensor_r(f)
-            if now:
-                tensor_a(b)
-            if b + 1 < ROUNDS:
-                tensor_h(b + 1)
-            if f < ROUNDS:
-                scalar_decay(f)
-            if b >= 1:
-                vector_mix(b - 1)
-            for unit in units[k:]:
-                quantise(*unit)
-            if b >= 1:
-                vector_add(b - 1)
+        for n in range(AHEAD):
+            scalar_prep(*units[n])
+        last = (0, PASSES - 1)
+        for n, (w, g) in enumerate(units):
+            f = 2 * (w - 1)
+            d = 2 * (w - 2)
+            products(*last)
+            last = (w, g)
+            if w < len(GROUPS) - 1:
+                if g == 0:
+                    at(scalar_decay, f - 2)
+                if g == 1:
+                    leave(w - 1, 2)
+                    leave(w - 1, 3)
+                if g == 2:
+                    at(scalar_tanh, f)
+                    at(scalar_decay, f - 1)
+                if g == 4:
+                    at(scalar_tanh, f + 1)
+                if n + AHEAD < len(units):
+                    scalar_prep(*units[n + AHEAD])
+                if g == 0:
+                    leave(w - 1, 0)
+                    leave(w - 1, 1)
+                vector_copies(w, g)
+                if g == 0:
+                    at(vector_lin, f - 1)
+                if g == 1:
+                    at(vector_add, d - 1)
+                if g == 2:
+                    at(vector_mix, d)
+                if g == 3:
+                    at(vector_lin, f)
+                if g == 4:
+                    at(vector_mix, d + 1)
+                quantise(w, g)
+                if g == 3:
+                    at(vector_add, d)
+                if g == 0:
+                    at(tensor_h, d)
+                if g == 1:
+                    at(tensor_r, f - 1)
+                    at(tensor_a, d)
+                if g == 3:
+                    at(tensor_h, d + 1)
+                    at(tensor_a, d + 1)
+                if g == 4:
+                    at(tensor_r, f)
+            else:
+                if g == 0:
+                    at(scalar_tanh, 14)
+                if g == 1:
+                    at(scalar_tanh, 15)
+                if g == 2:
+                    at(scalar_decay, 13)
+                if g == 3:
+                    at(scalar_decay, 14)
+                if g == 4:
+                    at(scalar_decay, 15)
+                if n + AHEAD < len(units):
+                    scalar_prep(*units[n + AHEAD])
+                if g == 0:
+                    at(scalar_decay, 12)
+                    leave(w - 1, 0)
+                if g == 1:
+                    leave(w - 1, 1)
+                vector_copies(w, g)
+                if g == 0:
+                    at(vector_lin, 13)
+                if g == 1:
+                    at(vector_lin, 14)
+                    at(vector_add, 11)
+                if g == 2:
+                    at(vector_mix, 12)
+                if g == 3:
+                    at(vector_lin, 15)
+                if g == 4:
+                    at(vector_mix, 13)
+                quantise(w, g)
+                if g == 3:
+                    at(vector_add, 12)
+                if g == 0:
+                    at(tensor_h, 12)
+                if g == 1:
+                    at(tensor_r, 13)
+                    at(tensor_a, 12)
+                if g == 2:
+                    at(tensor_r, 14)
+                if g == 3:
+                    at(tensor_h, 13)
+                    at(tensor_a, 13)
+                    at(tensor_r, 15)
+        products(*last)
+        leave(len(GROUPS) - 1, 0)
+        at(vector_add, 13)
+        at(tensor_h, 14)
+        at(tensor_a, 14)
+        at(vector_mix, 14)
+        leave(len(GROUPS) - 1, 1)
+        at(vector_add, 14)
+        at(tensor_h, 15)
+        at(tensor_a, 15)
+        at(vector_mix, 15)
+        at(vector_add, 15)

@@ -32,9 +32,10 @@ def group_list():
 
 
 GROUPS = group_list()
-GRP_BUFS = {SLAB: 6, 2 * P: 8, P: 6}
-WQ_BUFS = {SLAB: 4, 2 * P: 4, P: 4}
+FINAL = len(GROUPS) - 1
 AHEAD = 2
+GRP_BUFS = {SLAB: 6, 2 * P: 8}
+WQ_BUFS = 4
 
 
 def rounds_of(w):
@@ -48,7 +49,7 @@ def scalar_columns(w, g):
         return 3 * n // 4
     if w == 1:
         return n // 2 if g % 2 else n // 4
-    return n // 4 if g in (0, 2) else n // 2 if w < 7 else n // 4
+    return n // 4 if w >= FINAL - 1 or g in (0, 2) else n // 2
 
 
 def tile_ltccell_kernel(
@@ -63,7 +64,7 @@ def tile_ltccell_kernel(
         cgp = ctx.enter_context(tc.tile_pool(name="cgp", bufs=2))
         wqp = ctx.enter_context(tc.tile_pool(name="wqp", bufs=1))
         epi = ctx.enter_context(tc.tile_pool(name="epi", bufs=2))
-        psum = ctx.enter_context(tc.psum_pool(name="psum", bufs=2))
+        psum = ctx.enter_context(tc.psum_pool(name="psum", bufs=1))
 
         warm = const.tile([P, 1], F32, name="warm")
         nc.vector.memset(warm[:], 0.0)
@@ -92,10 +93,10 @@ def tile_ltccell_kernel(
 
         def load_c(src, passes):
             n = K_PASS * passes
-            tile = const.tile([P, BT, n], BF16, name="cn%d" % len(cn))
-            nc.sync.dma_start(out=tile[:], in_=src.rearrange("(i p) k -> p i k", p=P))
+            part = const.tile([P, BT, n], BF16, name="cn%d" % len(cn))
+            nc.sync.dma_start(out=part[:], in_=src.rearrange("(i p) k -> p i k", p=P))
             for g in range(passes):
-                cn.append(tile[:, :, K_PASS * g : K_PASS * (g + 1)])
+                cn.append(part[:, :, K_PASS * g : K_PASS * (g + 1)])
 
         chunks = [
             (c0, g, m) for c0 in range(0, H, SLAB) for m in range(2) for g in range(PASSES)
@@ -136,8 +137,7 @@ def tile_ltccell_kernel(
             cnf = cn[g].bitcast(F32).rearrange("p i (q u) -> p i u q", u=2)
             for half in range(2):
                 xt = psum.tile(
-                    [P, 2, 2, P], F32, name="xt%d_%d" % (g, half), tag=("RT", "DT")[half],
-                    bufs=1,
+                    [P, 2, 2, P], F32, name="xt%d_%d" % (g, half), tag=("RT", "DT")[half]
                 )
                 for il in range(2):
                     for u in range(2):
@@ -152,10 +152,7 @@ def tile_ltccell_kernel(
             for half in range(2):
                 dst = cgf[:, 256 * half : 256 * half + 256, :]
                 src = xts[(g, half)][:].rearrange("p u i b -> p (i b) u")
-                if half == 0:
-                    nc.vector.tensor_copy(out=dst, in_=src)
-                else:
-                    nc.scalar.copy(out=dst, in_=src)
+                (nc.vector.tensor_copy, nc.scalar.copy)[half](out=dst, in_=src)
             cgs[g] = cg
 
         def c_quantise(g):
@@ -179,19 +176,18 @@ def tile_ltccell_kernel(
                 ),
             )
 
-        def scalar_prep(w, g):
+        def scalar_regroup(w, g):
             n = GROUPS[w][2]
             grps[(w, g)] = grpp.tile(
                 [P, n, PACK], BF16, name="grp%d_%d" % (w, g), tag="grp%d" % n, align_bytes=64,
                 bufs=GRP_BUFS[n],
             )
-            for a in range(n - scalar_columns(w, g), n, 2 * P):
-                regroup(w, g, a, min(n, a + 2 * P), nc.scalar.copy)
+            for lo in range(n - scalar_columns(w, g), n, 2 * P):
+                regroup(w, g, lo, min(n, lo + 2 * P), nc.scalar.copy)
 
-        def vector_copies(w, g):
+        def vector_regroup(w, g):
             m, c0, n = GROUPS[w]
-            if scalar_columns(w, g) < n:
-                regroup(w, g, 0, n - scalar_columns(w, g), nc.vector.tensor_copy)
+            regroup(w, g, 0, n - scalar_columns(w, g), nc.vector.tensor_copy)
             if (c0 + n) % SLAB == 0:
                 ring["free"] += 1
             load_more()
@@ -199,10 +195,10 @@ def tile_ltccell_kernel(
         def quantise(w, g):
             m, c0, n = GROUPS[w]
             wq = wqp.tile(
-                [P, n], U32, name="wq%d_%d" % (w, g), tag="wq%d" % n, align_bytes=64, bufs=WQ_BUFS[n]
+                [P, n], U32, name="wq%d_%d" % (w, g), tag="wq%d" % n, align_bytes=64, bufs=WQ_BUFS
             )
             ws = wqp.tile(
-                [P, n], U8, name="ws%d_%d" % (w, g), tag="ws%d" % n, align_bytes=64, bufs=WQ_BUFS[n]
+                [P, n], U8, name="ws%d_%d" % (w, g), tag="ws%d" % n, align_bytes=64, bufs=WQ_BUFS
             )
             nc.vector.quantize_mx(
                 out=wq[:].bitcast(FP8X4), scales=ws[:],
@@ -254,7 +250,7 @@ def tile_ltccell_kernel(
             return cn[1 + r // 4][:, :, P * (r % 4) : P * (r % 4 + 1)]
 
         def tensor_h(r):
-            dt = psum.tile([P, BT, P], F32, name="dt%d" % r, tag="DT", bufs=1)
+            dt = psum.tile([P, BT, P], F32, name="dt%d" % r, tag="DT")
             nc.tensor.matmul(out=dt[:], lhsT=ident_b[:], rhs=h_of(r), start=True, stop=False)
             nc.tensor.matmul(
                 out=dt[:], lhsT=neg0[:],
@@ -264,7 +260,7 @@ def tile_ltccell_kernel(
             live[("dt", r)] = dt
 
         def tensor_r(r):
-            rt = psum.tile([P, BT, P], F32, name="rt%d" % r, tag="RT", bufs=1)
+            rt = psum.tile([P, BT, P], F32, name="rt%d" % r, tag="RT")
             for i in range(BT):
                 nc.tensor.transpose(
                     rt[:, i, :], live[("lin", r)][:, P * i : P * (i + 1)], ident_f[:]
@@ -293,39 +289,33 @@ def tile_ltccell_kernel(
             return (slice(0, 2), slice(2, 4)) if r == ROUNDS - 1 else (slice(0, BT),)
 
         def vector_mix(r):
-            q = r % 2
-            if r >= ROUNDS - 2:
-                live[("osb", r)] = []
-                for n, i in enumerate(parts_of(r)):
-                    o = epi.tile(
+            if r < ROUNDS - 2:
+                if r % 2 == 0:
+                    live["pair"] = epi.tile(
+                        [P, BT, 2 * P], F32, name="osb%d" % r, tag="osb", bufs=3
+                    )
+                outs = [live["pair"][:, :, P * (r % 2) : P * (r % 2 + 1)]]
+            else:
+                outs = [
+                    epi.tile(
                         [P, i.stop - i.start, P], F32, name="ose%d_%d" % (r, n), tag="ose", bufs=3
-                    )
-                    live[("osb", r)].append(o)
-                    nc.vector.scalar_tensor_tensor(
-                        out=o[:], in0=live[("dec", r)][:, i, :], scalar=-1.0,
-                        in1=live[("dt", r)][:, i, :], op0=ALU.add, op1=ALU.mult,
-                    )
-                return
-            if q == 0:
-                live["osb"] = epi.tile([P, BT, 2 * P], F32, name="osb%d" % r, tag="osb", bufs=3)
-            live[("osb", r)] = live["osb"]
-            nc.vector.scalar_tensor_tensor(
-                out=live["osb"][:, :, P * q : P * (q + 1)], in0=live[("dec", r)][:], scalar=-1.0,
-                in1=live[("dt", r)][:], op0=ALU.add, op1=ALU.mult,
-            )
+                    )[:]
+                    for n, i in enumerate(parts_of(r))
+                ]
+            live[("out", r)] = outs
+            for o, i in zip(outs, parts_of(r)):
+                nc.vector.scalar_tensor_tensor(
+                    out=o, in0=live[("dec", r)][:, i, :], scalar=-1.0,
+                    in1=live[("dt", r)][:, i, :], op0=ALU.add, op1=ALU.mult,
+                )
 
         def vector_add(r):
-            q = r % 2
-            osb = live[("osb", r)]
-            if r >= ROUNDS - 2:
-                for o, i in zip(osb, parts_of(r)):
-                    nc.vector.tensor_tensor(out=o[:], in0=o[:], in1=h_of(r)[:, i, :], op=ALU.add)
-                    nc.sync.dma_start(out=out_v[:, i, P * r : P * (r + 1)], in_=o[:])
-                return
-            mine = osb[:, :, P * q : P * (q + 1)]
-            nc.vector.tensor_tensor(out=mine, in0=mine, in1=h_of(r), op=ALU.add)
-            if q == 1:
-                nc.sync.dma_start(out=out_v[:, :, P * (r - 1) : P * (r + 1)], in_=osb[:])
+            for o, i in zip(live[("out", r)], parts_of(r)):
+                nc.vector.tensor_tensor(out=o, in0=o, in1=h_of(r)[:, i, :], op=ALU.add)
+                if r >= ROUNDS - 2:
+                    nc.sync.dma_start(out=out_v[:, i, P * r : P * (r + 1)], in_=o)
+            if r < ROUNDS - 2 and r % 2 == 1:
+                nc.sync.dma_start(out=out_v[:, :, P * (r - 1) : P * (r + 1)], in_=live["pair"][:])
 
         ctx.enter_context(tc.manual_schedule())
 
@@ -333,14 +323,14 @@ def tile_ltccell_kernel(
             for r in rounds_of(w):
                 mx_pass(r, GROUPS[w][0], g)
 
-        def leave(w, n):
-            if n < len(rounds_of(w)):
-                (scalar_a if GROUPS[w][0] else scalar_abs)(rounds_of(w)[n])
+        def leave(w, q):
+            if q < len(rounds_of(w)):
+                (scalar_a if GROUPS[w][0] else scalar_abs)(rounds_of(w)[q])
 
         units = [(w, g) for w in range(1, len(GROUPS)) for g in range(PASSES)]
         for g in range(PASSES):
-            scalar_prep(0, g)
-            vector_copies(0, g)
+            scalar_regroup(0, g)
+            vector_regroup(0, g)
             c_transpose(g)
             c_copies(g)
             quantise(0, g)
@@ -348,7 +338,7 @@ def tile_ltccell_kernel(
             if g >= 1:
                 products(0, g - 1)
             if g == 0:
-                pst = psum.tile([P, P], BF16, name="pst", tag="DT", bufs=1)
+                pst = psum.tile([P, P], BF16, name="pst", tag="DT")
                 nc.tensor.transpose(pst[:], vecs[:], ident_b[:])
                 cst = const.tile([P, P], F32, name="cst")
                 nc.vector.tensor_copy(out=cst[:], in_=pst[:])
@@ -384,107 +374,68 @@ def tile_ltccell_kernel(
             if 0 <= r < ROUNDS:
                 fn(r)
 
-        for n in range(AHEAD):
-            scalar_prep(*units[n])
+        for unit in units[:AHEAD]:
+            scalar_regroup(*unit)
+        vector_regroup(*units[0])
         last = (0, PASSES - 1)
-        for n, (w, g) in enumerate(units):
+        for step, (w, g) in enumerate(units):
             f = 2 * (w - 1)
             d = 2 * (w - 2)
             products(*last)
             last = (w, g)
-            if w < len(GROUPS) - 1:
-                if g == 0:
-                    at(scalar_decay, f - 2)
-                if g == 1:
-                    leave(w - 1, 2)
-                    leave(w - 1, 3)
-                if g == 2:
-                    at(scalar_tanh, f)
-                    at(scalar_decay, f - 1)
-                if g == 4:
-                    at(scalar_tanh, f + 1)
-                if n + AHEAD < len(units):
-                    scalar_prep(*units[n + AHEAD])
-                if g == 0:
-                    leave(w - 1, 0)
-                    leave(w - 1, 1)
-                vector_copies(w, g)
-                if g == 0:
-                    at(vector_lin, f - 1)
-                if g == 1:
-                    at(vector_add, d - 1)
-                if g == 2:
-                    at(vector_mix, d)
-                if g == 3:
-                    at(vector_lin, f)
-                if g == 4:
-                    at(vector_mix, d + 1)
-                quantise(w, g)
-                if g == 3:
-                    at(vector_add, d)
-                if g == 0:
-                    at(tensor_h, d)
-                if g == 1:
-                    at(tensor_r, f - 1)
-                    at(tensor_a, d)
-                if g == 3:
-                    at(tensor_h, d + 1)
-                    at(tensor_a, d + 1)
-                if g == 4:
-                    at(tensor_r, f)
-            else:
-                if g == 0:
-                    at(scalar_tanh, 14)
-                if g == 1:
-                    at(scalar_tanh, 15)
-                if g == 2:
-                    at(scalar_decay, 13)
-                if g == 3:
-                    at(scalar_decay, 14)
-                if g == 4:
-                    at(scalar_decay, 15)
-                if n + AHEAD < len(units):
-                    scalar_prep(*units[n + AHEAD])
-                if g == 0:
-                    at(scalar_decay, 12)
-                    leave(w - 1, 0)
-                if g == 1:
-                    leave(w - 1, 1)
-                vector_copies(w, g)
-                if g == 0:
-                    at(vector_lin, 13)
-                if g == 1:
-                    at(vector_lin, 14)
-                    at(vector_add, 11)
-                if g == 2:
-                    at(vector_mix, 12)
-                if g == 3:
-                    at(vector_lin, 15)
-                if g == 4:
-                    at(vector_mix, 13)
-                quantise(w, g)
-                if g == 3:
-                    at(vector_add, 12)
-                if g == 0:
-                    at(tensor_h, 12)
-                if g == 1:
-                    at(tensor_r, 13)
-                    at(tensor_a, 12)
-                if g == 2:
-                    at(tensor_r, 14)
-                if g == 3:
-                    at(tensor_h, 13)
-                    at(tensor_a, 13)
-                    at(tensor_r, 15)
+
+            if g == 0:
+                leave(w - 1, 0)
+                leave(w - 1, 1)
+            if g == 1:
+                at(scalar_tanh, f)
+                leave(w - 1, 2)
+            if g == 2:
+                at(scalar_decay, f - 1)
+                leave(w - 1, 3)
+            if g == 3:
+                at(scalar_tanh, f + 1)
+            if g == 4:
+                at(scalar_decay, f)
+            if step + AHEAD < len(units):
+                scalar_regroup(*units[step + AHEAD])
+
+            if step + 1 < len(units):
+                vector_regroup(*units[step + 1])
+            quantise(w, g)
+            if g == 0:
+                at(vector_add, d - 1)
+            if g == 2:
+                at(vector_lin, f)
+                at(vector_mix, d)
+            if g == 3:
+                at(vector_add, d)
+            if g == 4:
+                at(vector_lin, f + 1)
+                at(vector_mix, d + 1)
+
+            if g == 0:
+                at(tensor_h, d)
+            if g == 1:
+                at(tensor_r, f - 1)
+                at(tensor_a, d)
+            if g == 3:
+                at(tensor_h, d + 1)
+                at(tensor_r, f)
+                at(tensor_a, d + 1)
+
+        r = ROUNDS - 2
         products(*last)
-        leave(len(GROUPS) - 1, 0)
-        at(vector_add, 13)
-        at(tensor_h, 14)
-        at(tensor_a, 14)
-        at(vector_mix, 14)
-        leave(len(GROUPS) - 1, 1)
-        at(vector_add, 14)
-        at(tensor_h, 15)
-        at(tensor_a, 15)
-        at(vector_mix, 15)
-        at(vector_add, 15)
+        leave(FINAL, 0)
+        leave(FINAL, 1)
+        vector_add(r - 1)
+        tensor_r(r + 1)
+        tensor_h(r)
+        tensor_a(r)
+        scalar_decay(r + 1)
+        vector_mix(r)
+        vector_add(r)
+        tensor_h(r + 1)
+        tensor_a(r + 1)
+        vector_mix(r + 1)
+        vector_add(r + 1)

@@ -166,13 +166,13 @@ def tile_ltccell_kernel(
         wqs = {}
         live = {}
 
-        def regroup(w, g, lo, hi, engine_copy):
+        def regroup(w, g, lo, hi, engine_copy, run):
             m, c0, n = GROUPS[w]
             o = c0 % SLAB
             engine_copy(
-                out=grps[(w, g)][:, lo:hi, :].rearrange("p (c i) t -> p c t i", i=4),
+                out=grps[(w, g)][:, lo:hi, :].rearrange("p (c i) t -> p c t i", i=run),
                 in_=raws[(c0 // SLAB, g, m)][:, :, o + lo : o + hi].rearrange(
-                    "p t (c i) -> p c t i", i=4
+                    "p t (c i) -> p c t i", i=run
                 ),
             )
 
@@ -183,11 +183,11 @@ def tile_ltccell_kernel(
                 bufs=GRP_BUFS[n],
             )
             for lo in range(n - scalar_columns(w, g), n, 2 * P):
-                regroup(w, g, lo, min(n, lo + 2 * P), nc.scalar.copy)
+                regroup(w, g, lo, min(n, lo + 2 * P), nc.scalar.copy, 4)
 
         def vector_regroup(w, g):
             m, c0, n = GROUPS[w]
-            regroup(w, g, 0, n - scalar_columns(w, g), nc.vector.tensor_copy)
+            regroup(w, g, 0, n - scalar_columns(w, g), nc.vector.tensor_copy, 8)
             if (c0 + n) % SLAB == 0:
                 ring["free"] += 1
             load_more()

from contextlib import ExitStack

import concourse.mybir as mybir
from concourse.masks import make_identity

F32 = mybir.dt.float32
BF16 = mybir.dt.bfloat16
U32 = mybir.dt.uint32
U8 = mybir.dt.uint8
FP8X4 = mybir.dt.float8_e4m3fn_x4
ACT = mybir.ActivationFunctionType
ALU = mybir.AluOpType

P = 128
B, I, H = 512, 512, 2048
K = I + H
PACK = 4
K_PASS = P * PACK
PASSES = K // K_PASS
BT = B // P
ROUNDS = H // P
EPS = 1e-6
FLOPS = 2 * 2 * B * K * H

SLAB = 512
RAW_BUFS = 16


def group_list():
    groups = [(m, c0, SLAB) for c0 in range(0, H, SLAB) for m in range(2)][:-1]
    return groups + [(1, H - SLAB, 2 * P), (1, H - 2 * P, 2 * P)]


GROUPS = group_list()
FINAL = len(GROUPS) - 1
AHEAD = 2
GRP_BUFS = {SLAB: 6, 2 * P: 8}
WQ_BUFS = 4


def rounds_of(w):
    m, c0, n = GROUPS[w]
    return range(c0 // P, (c0 + n) // P)


def scalar_columns(w, g):
    n = GROUPS[w][2]
    if w == 0:
        return 3 * n // 4
    if w == 1:
        return n // 2 if g % 2 else n // 4
    return n // 4 if w >= FINAL - 1 or g in (0, 2) else n // 2


def tile_ltccell_kernel(
    tc, x, h, time_delta, W_mod, b_mod, W_tgt, b_tgt, log_tau, bias, out
):
    nc = tc.nc
    weights = (W_mod, W_tgt)
    with ExitStack() as ctx:
        const = ctx.enter_context(tc.tile_pool(name="const", bufs=1))
        rawp = ctx.enter_context(tc.tile_pool(name="rawp", bufs=1))
        grpp = ctx.enter_context(tc.tile_pool(name="grpp", bufs=1))
        cgp = ctx.enter_context(tc.tile_pool(name="cgp", bufs=2))
        wqp = ctx.enter_context(tc.tile_pool(name="wqp", bufs=1))
        epi = ctx.enter_context(tc.tile_pool(name="epi", bufs=2))
        psum = ctx.enter_context(tc.psum_pool(name="psum", bufs=1))

        warm = const.tile([P, 1], F32, name="warm")
        nc.vector.memset(warm[:], 0.0)
        nc.scalar.activation(out=warm[:], in_=warm[:], func=ACT.Exp)
        vecs = const.tile([P, P], BF16, name="vecs")
        nc.vector.memset(vecs[:], 0.0)
        for v, vec in enumerate((b_mod, b_tgt, log_tau, bias)):
            nc.scalar.dma_start(
                out=vecs[16 * v : 16 * v + 16, :], in_=vec.rearrange("(r c) -> r c", c=P)
            )
        nc.scalar.dma_start(
            out=vecs[64 : 64 + BT, :], in_=time_delta.rearrange("(i c) o -> i (c o)", c=P)
        )
        brow = const.tile([P, H], BF16, name="brow")
        nc.vector.memset(brow[:], 0.0)
        nc.scalar.dma_start(out=brow[0:1, :], in_=bias.rearrange("(o c) -> o c", o=1))
        neg0 = const.tile([P, P], BF16, name="neg0")
        nc.vector.memset(neg0[:], 0.0)
        nc.vector.memset(neg0[0:1, :], -1.0)
        ident_f = const.tile([P, P], F32, name="ident_f")
        make_identity(nc, ident_f[:])
        ident_b = const.tile([P, P], BF16, name="ident_b")
        make_identity(nc, ident_b[:])

        cn = []

        def load_c(src, passes):
            n = K_PASS * passes
            part = const.tile([P, BT, n], BF16, name="cn%d" % len(cn))
            nc.sync.dma_start(out=part[:], in_=src.rearrange("(i p) k -> p i k", p=P))
            for g in range(passes):
                cn.append(part[:, :, K_PASS * g : K_PASS * (g + 1)])

        chunks = [
            (c0, g, m) for c0 in range(0, H, SLAB) for m in range(2) for g in range(PASSES)
        ]
        raws = {}
        ring = {"next": 0, "free": RAW_BUFS}

        def load_more():
            while ring["next"] < len(chunks) and ring["free"] > 0:
                c0, g, m = chunks[ring["next"]]
                raw = rawp.tile(
                    [P, PACK, SLAB], BF16, name="raw%d" % ring["next"], tag="raw", bufs=RAW_BUFS
                )
                nc.sync.dma_start(
                    out=raw[:],
                    in_=weights[m][K_PASS * g : K_PASS * (g + 1), c0 : c0 + SLAB].rearrange(
                        "(p j) w -> p j w", j=PACK
                    ),
                )
                raws[(c0 // SLAB, g, m)] = raw
                if ring["next"] == 0:
                    load_c(x, 1)
                if ring["next"] == 1:
                    load_c(h[:, : H // 2], 2)
                if ring["next"] == 3:
                    load_c(h[:, H // 2 :], 2)
                ring["free"] -= 1
                ring["next"] += 1

        load_more()

        cq = []
        cs = []
        xts = {}
        cgs = {}

        def c_transpose(g):
            cnf = cn[g].bitcast(F32).rearrange("p i (q u) -> p i u q", u=2)
            for half in range(2):
                xt = psum.tile(
                    [P, 2, 2, P], F32, name="xt%d_%d" % (g, half), tag=("RT", "DT")[half]
                )
                for il in range(2):
                    for u in range(2):
                        nc.tensor.transpose(
                            xt[:, u, il, :], cnf[:, 2 * half + il, u, :], ident_f[:]
                        )
                xts[(g, half)] = xt

        def c_copies(g):
            cg = cgp.tile([P, B * PACK], BF16, name="cg%d" % g, tag="cg", align_bytes=64)
            cgf = cg[:].bitcast(F32).rearrange("p (b u) -> p b u", u=2)
            for half in range(2):
                dst = cgf[:, 256 * half : 256 * half + 256, :]
                src = xts[(g, half)][:].rearrange("p u i b -> p (i b) u")
                (nc.vector.tensor_copy, nc.scalar.copy)[half](out=dst, in_=src)
            cgs[g] = cg

        def c_quantise(g):
            cqg = const.tile([P, B], U32, name="cq%d" % g, align_bytes=64)
            csg = const.tile([P, B], U8, name="cs%d" % g, align_bytes=64)
            nc.vector.quantize_mx(out=cqg[:].bitcast(FP8X4), scales=csg[:], in_=cgs[g][:])
            cq.append(cqg)
            cs.append(csg)

        grps = {}
        wqs = {}
        live = {}

        def regroup(w, g, lo, hi, engine_copy, run):
            m, c0, n = GROUPS[w]
            o = c0 % SLAB
            engine_copy(
                out=grps[(w, g)][:, lo:hi, :].rearrange("p (c i) t -> p c t i", i=run),
                in_=raws[(c0 // SLAB, g, m)][:, :, o + lo : o + hi].rearrange(
                    "p t (c i) -> p c t i", i=run
                ),
            )

        def scalar_regroup(w, g):
            n = GROUPS[w][2]
            grps[(w, g)] = grpp.tile(
                [P, n, PACK], BF16, name="grp%d_%d" % (w, g), tag="grp%d" % n, align_bytes=64,
                bufs=GRP_BUFS[n],
            )
            for lo in range(n - scalar_columns(w, g), n, 2 * P):
                regroup(w, g, lo, min(n, lo + 2 * P), nc.scalar.copy, 4)

        def vector_regroup(w, g):
            m, c0, n = GROUPS[w]
            regroup(w, g, 0, n - scalar_columns(w, g), nc.vector.tensor_copy, 8)
            if (c0 + n) % SLAB == 0:
                ring["free"] += 1
            load_more()

        def quantise(w, g):
            m, c0, n = GROUPS[w]
            wq = wqp.tile(
                [P, n], U32, name="wq%d_%d" % (w, g), tag="wq%d" % n, align_bytes=64, bufs=WQ_BUFS
            )
            ws = wqp.tile(
                [P, n], U8, name="ws%d_%d" % (w, g), tag="ws%d" % n, align_bytes=64, bufs=WQ_BUFS
            )
            nc.vector.quantize_mx(
                out=wq[:].bitcast(FP8X4), scales=ws[:],
                in_=grps[(w, g)][:].rearrange("p w t -> p (w t)"),
            )
            for i, r in enumerate(rounds_of(w)):
                wqs[(r, g, m)] = (wq, ws, P * i)

        def mx_pass(r, m, g):
            if g == 0:
                live[("z", r, m)] = psum.tile(
                    [P, B], F32, name="ps%d_%d" % (m, r), tag="Z", bufs=6
                )
            wq, ws, o = wqs[(r, g, m)]
            nc.tensor.matmul_mx(
                out=live[("z", r, m)][:],
                lhsT=wq[:, o : o + P].bitcast(FP8X4), lhsT_scale=ws[:, o : o + P],
                rhs=cq[g][:].bitcast(FP8X4), rhs_scale=cs[g][:],
                start=(g == 0), stop=(g == PASSES - 1),
            )

        def scalar_a(r):
            a = epi.tile([P, B], F32, name="a%d" % r, tag="a", bufs=6)
            nc.scalar.activation(
                out=a[:], in_=live[("z", r, 1)][:], func=ACT.Tanh, bias=nbt[:, r : r + 1], scale=-1.0
            )
            live[("a", r)] = a

        def scalar_abs(r):
            u = epi.tile([P, B], F32, name="u%d" % r, tag="u", bufs=6)
            nc.scalar.activation(
                out=u[:], in_=live[("z", r, 0)][:], func=ACT.Abs, bias=cst[:, r : r + 1]
            )
            live[("u", r)] = u

        def scalar_tanh(r):
            u = live[("u", r)]
            nc.scalar.activation(out=u[:], in_=u[:], func=ACT.Tanh, bias=epsc[:])

        def vector_lin(r):
            lin = epi.tile([P, B], F32, name="lin%d" % r, tag="lin")
            nc.vector.tensor_scalar(
                out=lin[:], in0=live[("u", r)][:], scalar1=c1[:, r : r + 1],
                scalar2=c0t[:, r : r + 1], op0=ALU.mult, op1=ALU.add,
            )
            live[("lin", r)] = lin

        def h_of(r):
            return cn[1 + r // 4][:, :, P * (r % 4) : P * (r % 4 + 1)]

        def tensor_h(r):
            dt = psum.tile([P, BT, P], F32, name="dt%d" % r, tag="DT")
            nc.tensor.matmul(out=dt[:], lhsT=ident_b[:], rhs=h_of(r), start=True, stop=False)
            nc.tensor.matmul(
                out=dt[:], lhsT=neg0[:],
                rhs=brow[:, P * r : P * (r + 1)].unsqueeze(1).to_broadcast([P, BT, P]),
                start=False, stop=False,
            )
            live[("dt", r)] = dt

        def tensor_r(r):
            rt = psum.tile([P, BT, P], F32, name="rt%d" % r, tag="RT")
            for i in range(BT):
                nc.tensor.transpose(
                    rt[:, i, :], live[("lin", r)][:, P * i : P * (i + 1)], ident_f[:]
                )
            live[("rt", r)] = rt

        def tensor_a(r):
            for i in range(BT):
                nc.tensor.matmul(
                    out=live[("dt", r)][:, i, :], lhsT=live[("a", r)][:, P * i : P * (i + 1)],
                    rhs=ident_f[:], is_transpose=True, start=False, stop=(i == BT - 1),
                )

        def scalar_decay(r):
            dec = epi.tile([P, BT, P], F32, name="dec%d" % r, tag="dec", bufs=4)
            for i in range(BT):
                nc.scalar.activation(
                    out=dec[:, i, :], in_=live[("rt", r)][:, i, :], func=ACT.Exp,
                    scale=cst[:, 64 + i : 65 + i],
                )
            live[("dec", r)] = dec

        out_v = out.rearrange("(i p) c -> p i c", p=P)

        def parts_of(r):
            return (slice(0, 2), slice(2, 4)) if r == ROUNDS - 1 else (slice(0, BT),)

        def vector_mix(r):
            if r < ROUNDS - 2:
                if r % 2 == 0:
                    live["pair"] = epi.tile(
                        [P, BT, 2 * P], F32, name="osb%d" % r, tag="osb", bufs=3
                    )
                outs = [live["pair"][:, :, P * (r % 2) : P * (r % 2 + 1)]]
            else:
                outs = [
                    epi.tile(
                        [P, i.stop - i.start, P], F32, name="ose%d_%d" % (r, n), tag="ose", bufs=3
                    )[:]
                    for n, i in enumerate(parts_of(r))
                ]
            live[("out", r)] = outs
            for o, i in zip(outs, parts_of(r)):
                nc.vector.scalar_tensor_tensor(
                    out=o, in0=live[("dec", r)][:, i, :], scalar=-1.0,
                    in1=live[("dt", r)][:, i, :], op0=ALU.add, op1=ALU.mult,
                )

        def vector_add(r):
            for o, i in zip(live[("out", r)], parts_of(r)):
                nc.vector.tensor_tensor(out=o, in0=o, in1=h_of(r)[:, i, :], op=ALU.add)
                if r >= ROUNDS - 2:
                    nc.sync.dma_start(out=out_v[:, i, P * r : P * (r + 1)], in_=o)
            if r < ROUNDS - 2 and r % 2 == 1:
                nc.sync.dma_start(out=out_v[:, :, P * (r - 1) : P * (r + 1)], in_=live["pair"][:])

        ctx.enter_context(tc.manual_schedule())

        def products(w, g):
            for r in rounds_of(w):
                mx_pass(r, GROUPS[w][0], g)

        def leave(w, q):
            if q < len(rounds_of(w)):
                (scalar_a if GROUPS[w][0] else scalar_abs)(rounds_of(w)[q])

        units = [(w, g) for w in range(1, len(GROUPS)) for g in range(PASSES)]
        for g in range(PASSES):
            scalar_regroup(0, g)
            vector_regroup(0, g)
            c_transpose(g)
            c_copies(g)
            quantise(0, g)
            c_quantise(g)
            if g >= 1:
                products(0, g - 1)
            if g == 0:
                pst = psum.tile([P, P], BF16, name="pst", tag="DT")
                nc.tensor.transpose(pst[:], vecs[:], ident_b[:])
                cst = const.tile([P, P], F32, name="cst")
                nc.vector.tensor_copy(out=cst[:], in_=pst[:])
            if g == 1:
                itau = const.tile([P, 16], F32, name="itau")
                nc.scalar.activation(out=itau[:], in_=cst[:, 32:48], func=ACT.Exp, scale=-1.0)
            if g == 2:
                t1n = const.tile([P, 16], F32, name="t1n")
                nc.vector.tensor_scalar(
                    out=t1n[:], in0=itau[:], scalar1=-EPS, scalar2=-1.0, op0=ALU.mult, op1=ALU.add
                )
                nk0 = const.tile([P, 16], F32, name="nk0")
                nc.vector.reciprocal(out=nk0[:], in_=t1n[:])
                c1 = const.tile([P, 16], F32, name="c1")
                nc.vector.scalar_tensor_tensor(
                    out=c1[:], in0=nk0[:], scalar=-1.0, in1=nk0[:], op0=ALU.mult, op1=ALU.mult
                )
                nbt = const.tile([P, 16], F32, name="nbt")
                nc.vector.tensor_scalar(
                    out=nbt[:], in0=cst[:, 16:32], scalar1=-1.0, scalar2=None, op0=ALU.mult
                )
                c0t = const.tile([P, 16], F32, name="c0t")
                nc.vector.scalar_tensor_tensor(
                    out=c0t[:], in0=nk0[:], scalar=EPS, in1=itau[:], op0=ALU.mult, op1=ALU.add
                )
                nc.vector.tensor_tensor(out=c0t[:], in0=c0t[:], in1=nk0[:], op=ALU.mult)
                epsc = const.tile([P, 1], F32, name="epsc")
                nc.vector.tensor_scalar(
                    out=epsc[:], in0=itau[:, 0:1], scalar1=0.0, scalar2=EPS, op0=ALU.mult, op1=ALU.add
                )

        def at(fn, r):
            if 0 <= r < ROUNDS:
                fn(r)

        for unit in units[:AHEAD]:
            scalar_regroup(*unit)
        vector_regroup(*units[0])
        last = (0, PASSES - 1)
        for step, (w, g) in enumerate(units):
            f = 2 * (w - 1)
            d = 2 * (w - 2)
            products(*last)
            last = (w, g)

            if g == 0:
                leave(w - 1, 0)
                leave(w - 1, 1)
            if g == 1:
                at(scalar_tanh, f)
                leave(w - 1, 2)
            if g == 2:
                at(scalar_decay, f - 1)
                leave(w - 1, 3)
            if g == 3:
                at(scalar_tanh, f + 1)
            if g == 4:
                at(scalar_decay, f)
            if step + AHEAD < len(units):
                scalar_regroup(*units[step + AHEAD])

            if step + 1 < len(units):
                vector_regroup(*units[step + 1])
            quantise(w, g)
            if g == 0:
                at(vector_add, d - 1)
            if g == 2:
                at(vector_lin, f)
                at(vector_mix, d)
            if g == 3:
                at(vector_add, d)
            if g == 4:
                at(vector_lin, f + 1)
                at(vector_mix, d + 1)

            if g == 0:
                at(tensor_h, d)
            if g == 1:
                at(tensor_r, f - 1)
                at(tensor_a, d)
            if g == 3:
                at(tensor_h, d + 1)
                at(tensor_r, f)
                at(tensor_a, d + 1)

        r = ROUNDS - 2
        products(*last)
        leave(FINAL, 0)
        leave(FINAL, 1)
        vector_add(r - 1)
        tensor_r(r + 1)
        tensor_h(r)
        tensor_a(r)
        scalar_decay(r + 1)
        vector_mix(r)
        vector_add(r)
        tensor_h(r + 1)
        tensor_a(r + 1)
        vector_mix(r + 1)
        vector_add(r + 1)
